import numpy as np
import ml_dtypes


def mxq(x, axis, fmt="e4m3"):
    dtype, down = {"e4m3": (ml_dtypes.float8_e4m3fn, 7), "e5m2": (ml_dtypes.float8_e5m2, 14)}[fmt]
    v = np.moveaxis(np.asarray(x, np.float32).astype(ml_dtypes.bfloat16).astype(np.float64), axis, -1)
    blocks = v.reshape(v.shape[:-1] + (-1, 32))
    amax = np.abs(blocks).max(-1, keepdims=True)
    byte = np.maximum(np.where(amax > 0, np.frexp(amax)[1] - 1 + 127, 0) - down, 1)
    scale = np.exp2(byte - 127.0)
    codes = (blocks / scale).astype(np.float32).astype(dtype).astype(np.float64)
    return np.moveaxis((codes * scale).reshape(v.shape), -1, axis)


WIDE = False


def mx_kscale(k):
    if not WIDE:
        return np.ones(k)
    levels = np.array([10, -10, 5, -5, 0])
    a = np.random.permutation(np.resize(levels, k // 512 * 4)).reshape(k // 512, 4)
    idx = np.arange(k)
    return np.exp2(a[idx // 512, idx % 128 // 32])


BF16 = ml_dtypes.bfloat16


def bf(x):
    return np.asarray(x, np.float32).astype(BF16)


def f64(x):
    return np.asarray(x).astype(np.float64)


B, N, IN_DIM, OUT_DIM, NUM_F = 2, 256, 1024, 768, 8


def silu(v):
    return v / (1.0 + np.exp(-v))


def setup_inputs():
    t = mx_kscale(IN_DIM)
    return {"x": bf(np.random.standard_normal((B, N, IN_DIM))),
            "base_weight": bf(np.random.standard_normal((OUT_DIM, IN_DIM)) / np.sqrt(IN_DIM)),
            "grid": bf(np.arange(NUM_F) + 1.0),
            "scale_sp": bf(1.0 + 0.1 * np.random.standard_normal(OUT_DIM)),
            "coef": bf(np.random.uniform(size=(IN_DIM, NUM_F)) * t[:, None]),
            "conv_w": bf(np.random.standard_normal((NUM_F, OUT_DIM, IN_DIM)) / np.sqrt(IN_DIM) / t[None, None, :]),
            "conv_b": bf(np.random.standard_normal((NUM_F, OUT_DIM)) * 0.1)}


def reference(x, base_weight, grid, scale_sp, coef, conv_w, conv_b):
    x = f64(x)
    b, n, d = x.shape
    xf = x.reshape(b * n, d)
    base_out = mxq(silu(xf), 1, "e4m3") @ mxq(f64(base_weight), 1, "e4m3").T
    s = np.sin(xf[:, None, :] * f64(grid)[None, :, None]) * f64(coef).T[None, :, :]
    sq = mxq(s, 2, "e4m3")
    wq = mxq(f64(conv_w), 2, "e4m3")
    spline = np.matmul(sq.transpose(1, 0, 2), wq.transpose(0, 2, 1)).transpose(1, 0, 2) + f64(conv_b)[None, :, :]
    out = base_out + spline.sum(axis=1) * f64(scale_sp)
    return out.reshape(b, n, OUT_DIM)

@@ -1,0 +1,230 @@
+import math
+from contextlib import ExitStack
+
+import concourse.mybir as mybir
+from concourse.masks import make_identity
+
+F32 = mybir.dt.float32
+BF16 = mybir.dt.bfloat16
+I32 = mybir.dt.int32
+U32 = mybir.dt.uint32
+U8 = mybir.dt.uint8
+FP8X4 = mybir.dt.float8_e4m3fn_x4
+ALU = mybir.AluOpType
+ACT = mybir.ActivationFunctionType
+
+P = 128
+TOK = 512
+K = 1024
+O = 768
+NF = 8
+OT = O // P
+TT = TOK // P
+G = K // 512
+CH = TOK * 4
+
+FLOPS = 2 * TOK * O * K * (NF + 1)
+
+GROUPED = (5, 13, 14, 15)
+VEC_EXIT_EVERY = 0
+
+
+def tile_efficient_skan_batch_kernel(tc, x, base_weight, grid, scale_sp, coef, conv_w, conv_b, out):
+    nc = tc.nc
+    with ExitStack() as ctx:
+        const = ctx.enter_context(tc.tile_pool(name="const", bufs=1))
+        work = ctx.enter_context(tc.tile_pool(name="work", bufs=2))
+        psum = ctx.enter_context(tc.psum_pool(name="psum", bufs=1))
+
+        x_sb = const.tile([P, TT, K], BF16)
+        x_view = x.rearrange("b (h p) k -> p (b h) k", p=P)
+        for t in range(TT):
+            nc.sync.dma_start(out=x_sb[:, t, :], in_=x_view[:, t, :])
+
+        grid_bc = const.tile([P, NF], BF16)
+        nc.scalar.dma_start(out=grid_bc[:], in_=grid.partition_broadcast(P))
+        coef_raw = const.tile([P, 4, 2 * NF], BF16)
+        with nc.allow_non_contiguous_dma(reason="coef rows in runs of 32 bytes"):
+            nc.scalar.dma_start(out=coef_raw[:], in_=coef.rearrange("(b p e) f -> p b (e f)", b=4, p=P, e=2))
+        brow = const.tile([P, O], BF16)
+        nc.vector.memset(brow[:], 0.0)
+        nc.scalar.dma_start(out=brow[0:NF, :], in_=conv_b)
+        nc.scalar.dma_start(out=brow[NF : NF + 1, :], in_=scale_sp.rearrange("(a o) -> a o", a=1))
+
+        ident = const.tile([P, P], F32)
+        make_identity(nc, ident[:])
+        identb = const.tile([P, P], BF16)
+        make_identity(nc, identb[:])
+
+        def load_weights(m):
+            w_raw = work.tile([P, OT, K], BF16, tag="w_raw", bufs=3, name="w_raw")
+            src = base_weight if m == 0 else conv_w[m - 1]
+            nc.sync.dma_start(out=w_raw[:], in_=src.rearrange("(t p) k -> p t k", p=P))
+            return w_raw
+
+        g2 = const.tile([P, NF], F32)
+        nc.vector.tensor_scalar(out=g2[:], in0=grid_bc[:], scalar1=1.0 / (2.0 * math.pi), scalar2=None, op0=ALU.mult)
+        coeft = const.tile([P, NF, 8], F32)
+        nc.vector.tensor_copy(
+            out=coeft[:].rearrange("p f (b e) -> p f b e", b=4, e=2),
+            in_=coef_raw[:].rearrange("p b (e f) -> p f b e", e=2, f=NF),
+        )
+
+        xw = x_sb[:].rearrange("p t k -> p (t k)").bitcast(F32)
+        xg = const.tile([P, G * CH], BF16, align_bytes=64)
+        xgw = xg[:].bitcast(F32).rearrange("p (g t u) -> p g t u", g=G, t=TOK, u=2)
+        xp = const.tile([P, G * CH], BF16, align_bytes=64)
+        xpv = xp[:].rearrange("p (c e t) -> p c e t", c=4, e=2, t=TOK)
+        for t in range(TT):
+            bank = psum.tile([P, 4, P], F32, tag="tp", bufs=2, name="bank")
+            for b in range(4):
+                nc.tensor.transpose(bank[:, b, :], xw[:, t * 512 + b * P : t * 512 + (b + 1) * P], ident[:])
+            nc.scalar.copy(
+                out=xgw[:, :, t * P : (t + 1) * P, :],
+                in_=bank[:].rearrange("p (g u) t -> p g t u", g=G, u=2),
+            )
+            nc.vector.tensor_copy(
+                out=xpv[:, :, :, t * P : (t + 1) * P],
+                in_=bank[:].rearrange("p c t -> p (c t)").bitcast(BF16).rearrange("p (c t e) -> p c e t", c=4, t=P, e=2),
+            )
+
+        bankb = psum.tile([P, OT, P], BF16, tag="tp", bufs=2, name="bankb")
+        for ot in range(OT):
+            nc.tensor.transpose(bankb[:, ot, :], brow[:, ot * P : (ot + 1) * P], identb[:])
+        bs = const.tile([P, OT, 16], F32)
+        nc.vector.tensor_copy(out=bs[:, :, 0 : NF + 1], in_=bankb[:, :, 0 : NF + 1])
+        cb = const.tile([P, OT], F32)
+        nc.vector.tensor_reduce(out=cb[:], in_=bs[:, :, 0:NF], axis=mybir.AxisListType.X, op=ALU.add)
+        scl = const.tile([P, OT], F32)
+        nc.vector.tensor_copy(out=scl[:], in_=bs[:, :, NF])
+        cbs = const.tile([P, OT], F32)
+        nc.vector.tensor_tensor(out=cbs[:], in0=cb[:], in1=scl[:], op=ALU.mult)
+
+        def weight_stage(m, w_raw):
+            ww = w_raw[:].rearrange("p t k -> p (t k)").bitcast(F32)
+            wg = work.tile([P, OT * 1024], BF16, tag="wg", bufs=2, name="wg", align_bytes=64)
+            wgw = wg[:].bitcast(F32)
+            wc = work.tile([P, OT * 256], U32, tag="wc", bufs=2, name="wc", align_bytes=64)
+            ws = work.tile([P, OT * 256], U8, tag="ws", bufs=2, name="ws", align_bytes=64)
+            for ot in range(OT):
+                bank = psum.tile([P, 4, P], F32, tag="tp", bufs=2, name="bank")
+                for b in range(4):
+                    nc.tensor.transpose(bank[:, b, :], ww[:, ot * 512 + b * P : ot * 512 + (b + 1) * P], ident[:])
+                dst = wgw[:, ot * 512 : (ot + 1) * 512].rearrange("p (g o u) -> p g o u", g=G, o=P, u=2)
+                src = bank[:].rearrange("p (g u) o -> p g o u", g=G, u=2)
+                if VEC_EXIT_EVERY and (m * OT + ot) % VEC_EXIT_EVERY == 0:
+                    nc.vector.tensor_copy(out=dst, in_=src)
+                else:
+                    nc.scalar.copy(out=dst, in_=src)
+                if ot % 2 == 1:
+                    q = ot // 2
+                    nc.vector.quantize_mx(
+                        out=wc[:, q * 512 : (q + 1) * 512].bitcast(FP8X4),
+                        scales=ws[:, q * 512 : (q + 1) * 512],
+                        in_=wg[:, q * 2048 : (q + 1) * 2048],
+                    )
+            return wc, ws
+
+        def act_tiles():
+            sc = work.tile([P, G * TOK], U32, tag="sc", bufs=3, name="sc", align_bytes=64)
+            ss = work.tile([P, G * TOK], U8, tag="ss", bufs=3, name="ss", align_bytes=64)
+            return sc, ss
+
+        def silu_stage():
+            sc, ss = act_tiles()
+            sl = const.tile([P, G * CH], BF16, align_bytes=64)
+            nc.scalar.activation(out=sl[:], in_=xg[:], func=ACT.Silu)
+            nc.vector.quantize_mx(out=sc[:].bitcast(FP8X4), scales=ss[:], in_=sl[:])
+            return sc, ss
+
+        def sine_stage(f):
+            sc, ss = act_tiles()
+            gf = g2[:, f : f + 1]
+            for g in range(G):
+                grouped = (f * G + g) in GROUPED
+                xin = (xg if grouped else xp)[:, g * CH : (g + 1) * CH]
+                n = work.tile([P, CH], I32, tag="n", bufs=2, name="n")
+                nc.vector.tensor_scalar(out=n[:], in0=xin, scalar1=gf, scalar2=None, op0=ALU.mult)
+                r = work.tile([P, CH], F32, tag="r", bufs=3, name="r")
+                nc.vector.scalar_tensor_tensor(out=r[:], in0=xin, scalar=gf, in1=n[:], op0=ALU.mult, op1=ALU.subtract)
+                nc.scalar.activation(out=r[:], in_=r[:], func=ACT.Sin, scale=2.0 * math.pi)
+                sg = work.tile([P, CH], BF16, tag="sg", bufs=2, name="sg", align_bytes=64)
+                if grouped:
+                    nc.vector.tensor_tensor(
+                        out=sg[:].rearrange("p (t j) -> p t j", j=4),
+                        in0=r[:].rearrange("p (t j) -> p t j", j=4),
+                        in1=coeft[:, f, g * 4 : (g + 1) * 4].unsqueeze(1).to_broadcast([P, TOK, 4]),
+                        op=ALU.mult,
+                    )
+                else:
+                    sp = work.tile([P, CH], BF16, tag="sp", bufs=2, name="sp")
+                    for j in range(4):
+                        nc.vector.tensor_scalar(
+                            out=sp[:, j * TOK : (j + 1) * TOK],
+                            in0=r[:, j * TOK : (j + 1) * TOK],
+                            scalar1=coeft[:, f, g * 4 + j : g * 4 + j + 1],
+                            scalar2=None,
+                            op0=ALU.mult,
+                        )
+                    nc.scalar.copy(
+                        out=sg[:].rearrange("p (c i j) -> p c j i", i=4, j=4),
+                        in_=sp[:].rearrange("p (j c i) -> p c j i", j=4, i=4),
+                    )
+                nc.vector.quantize_mx(
+                    out=sc[:, g * TOK : (g + 1) * TOK].bitcast(FP8X4),
+                    scales=ss[:, g * TOK : (g + 1) * TOK],
+                    in_=sg[:],
+                )
+            return sc, ss
+
+        def mx_stage(acc, wc, ws, sc, ss, first, last):
+            for g in range(G):
+                for ot in range(OT):
+                    cols = slice((ot * G + g) * P, (ot * G + g + 1) * P)
+                    nc.tensor.matmul_mx(
+                        out=acc[ot][:],
+                        lhsT=wc[:, cols].bitcast(FP8X4),
+                        lhsT_scale=ws[:, cols],
+                        rhs=sc[:, g * TOK : (g + 1) * TOK].bitcast(FP8X4),
+                        rhs_scale=ss[:, g * TOK : (g + 1) * TOK],
+                        start=(first and g == 0),
+                        stop=(last and g == G - 1),
+                    )
+
+        def new_acc():
+            return [psum.tile([P, TOK], F32, tag="acc%d" % ot, bufs=1, name="acc%d" % ot) for ot in range(OT)]
+
+        raws = [load_weights(0), load_weights(1)]
+        wc, ws = weight_stage(0, raws[0])
+        sc, ss = silu_stage()
+        acc = new_acc()
+        mx_stage(acc, wc, ws, sc, ss, True, True)
+        base_c = const.tile([P, OT, TOK], F32)
+        for ot in range(OT):
+            nc.scalar.activation(out=base_c[:, ot, :], in_=acc[ot][:], func=ACT.Identity, bias=cbs[:, ot : ot + 1], scale=1.0)
+
+        acc = new_acc()
+        for f in range(NF):
+            if f + 2 <= NF:
+                raws.append(load_weights(f + 2))
+            wc, ws = weight_stage(f + 1, raws[f + 1])
+            sc, ss = sine_stage(f)
+            mx_stage(acc, wc, ws, sc, ss, f == 0, f == NF - 1)
+
+        out_sb = const.tile([P, TT, O], F32)
+        out_view = out.rearrange("b (h p) o -> p (b h) o", p=P)
+        for ot in range(OT):
+            y = work.tile([P, TOK], F32, tag="y", bufs=3, name="y")
+            nc.vector.scalar_tensor_tensor(
+                out=y[:], in0=acc[ot][:], scalar=scl[:, ot : ot + 1], in1=base_c[:, ot, :], op0=ALU.mult, op1=ALU.add
+            )
+            bank = psum.tile([P, 4, P], F32, tag="tp", bufs=2, name="bank")
+            for t in range(TT):
+                nc.tensor.transpose(bank[:, t, :], y[:, t * P : (t + 1) * P], ident[:])
+            if ot % 2 == 0:
+                nc.scalar.copy(out=out_sb[:, :, ot * P : (ot + 1) * P], in_=bank[:])
+            else:
+                nc.vector.tensor_copy(out=out_sb[:, :, ot * P : (ot + 1) * P], in_=bank[:])
+            if ot % 3 == 2:
+                h = ot // 3
+                nc.sync.dma_start(out=out_view[:, :, h * 384 : (h + 1) * 384], in_=out_sb[:, :, h * 384 : (h + 1) * 384])

@@ -36,10 +36,11 @@ def tile_efficient_skan_batch_kernel(tc, x, base_weight, grid, scale_sp, coef, c
         work = ctx.enter_context(tc.tile_pool(name="work", bufs=2))
         psum = ctx.enter_context(tc.psum_pool(name="psum", bufs=1))
 
-        x_sb = const.tile([P, TT, K], BF16)
-        x_view = x.rearrange("b (h p) k -> p (b h) k", p=P)
-        for t in range(TT):
-            nc.sync.dma_start(out=x_sb[:, t, :], in_=x_view[:, t, :])
+        x_sb = const.tile([P, G, TT, K // G], BF16)
+        x_view = x.rearrange("b (h p) (g k) -> p g (b h) k", p=P, g=G)
+        for g in range(G):
+            for h in range(2):
+                nc.sync.dma_start(out=x_sb[:, g, 2 * h : 2 * h + 2, :], in_=x_view[:, g, 2 * h : 2 * h + 2, :])
 
         grid_bc = const.tile([P, NF], BF16)
         nc.scalar.dma_start(out=grid_bc[:], in_=grid.partition_broadcast(P))
@@ -70,23 +71,19 @@ def tile_efficient_skan_batch_kernel(tc, x, base_weight, grid, scale_sp, coef, c
             in_=coef_raw[:].rearrange("p b (e f) -> p f b e", e=2, f=NF),
         )
 
-        xw = x_sb[:].rearrange("p t k -> p (t k)").bitcast(F32)
-        xg = const.tile([P, G * CH], BF16, align_bytes=64)
-        xgw = xg[:].bitcast(F32).rearrange("p (g t u) -> p g t u", g=G, t=TOK, u=2)
+        xw = x_sb[:].rearrange("p g t k -> p (g t k)").bitcast(F32).rearrange("p (g t u w) -> p g u t w", g=G, t=TT, u=2)
         xp = const.tile([P, G * CH], BF16, align_bytes=64)
-        xpv = xp[:].rearrange("p (c e t) -> p c e t", c=4, e=2, t=TOK)
-        for t in range(TT):
-            bank = psum.tile([P, 4, P], F32, tag="tp", bufs=2, name="bank")
-            for b in range(4):
-                nc.tensor.transpose(bank[:, b, :], xw[:, t * 512 + b * P : t * 512 + (b + 1) * P], ident[:])
-            nc.scalar.copy(
-                out=xgw[:, :, t * P : (t + 1) * P, :],
-                in_=bank[:].rearrange("p (g u) t -> p g t u", g=G, u=2),
-            )
-            nc.vector.tensor_copy(
-                out=xpv[:, :, :, t * P : (t + 1) * P],
-                in_=bank[:].rearrange("p c t -> p (c t)").bitcast(BF16).rearrange("p (c t e) -> p c e t", c=4, t=P, e=2),
-            )
+        for g in range(G):
+            for u in range(2):
+                bank = psum.tile([P, TOK], F32, tag="acc%d" % (2 * g + u), bufs=1, name="bank")
+                for t in range(TT):
+                    nc.tensor.transpose(bank[:, t * P : (t + 1) * P], xw[:, g, u, t, :], ident[:])
+                dst = xp[:, (2 * g + u) * 1024 : (2 * g + u + 1) * 1024].rearrange("p (e t) -> p e t", e=2)
+                src = bank[:].bitcast(BF16).rearrange("p (t e) -> p e t", e=2)
+                if u == 0:
+                    nc.vector.tensor_copy(out=dst, in_=src)
+                else:
+                    nc.scalar.copy(out=dst, in_=src)
 
         bankb = psum.tile([P, OT, P], BF16, tag="tp", bufs=2, name="bankb")
         for ot in range(OT):
@@ -133,7 +130,12 @@ def tile_efficient_skan_batch_kernel(tc, x, base_weight, grid, scale_sp, coef, c
         def silu_stage():
             sc, ss = act_tiles()
             sl = const.tile([P, G * CH], BF16, align_bytes=64)
-            nc.scalar.activation(out=sl[:], in_=xg[:], func=ACT.Silu)
+            for g in range(G):
+                nc.scalar.activation(
+                    out=sl[:, g * CH : (g + 1) * CH].rearrange("p (c i j) -> p c j i", i=4, j=4),
+                    in_=xp[:, g * CH : (g + 1) * CH].rearrange("p (j c i) -> p c j i", j=4, i=4),
+                    func=ACT.Silu,
+                )
             nc.vector.quantize_mx(out=sc[:].bitcast(FP8X4), scales=ss[:], in_=sl[:])
             return sc, ss
 
@@ -142,17 +144,17 @@ def tile_efficient_skan_batch_kernel(tc, x, base_weight, grid, scale_sp, coef, c
             gf = g2[:, f : f + 1]
             for g in range(G):
                 grouped = (f * G + g) in GROUPED
-                xin = (xg if grouped else xp)[:, g * CH : (g + 1) * CH]
+                xin = xp[:, g * CH : (g + 1) * CH]
                 n = work.tile([P, CH], I32, tag="n", bufs=2, name="n")
                 nc.vector.tensor_scalar(out=n[:], in0=xin, scalar1=gf, scalar2=None, op0=ALU.mult)
-                r = work.tile([P, CH], F32, tag="r", bufs=3, name="r")
+                r = work.tile([P, CH], F32, tag="r", bufs=4, name="r")
                 nc.vector.scalar_tensor_tensor(out=r[:], in0=xin, scalar=gf, in1=n[:], op0=ALU.mult, op1=ALU.subtract)
                 nc.scalar.activation(out=r[:], in_=r[:], func=ACT.Sin, scale=2.0 * math.pi)
                 sg = work.tile([P, CH], BF16, tag="sg", bufs=2, name="sg", align_bytes=64)
                 if grouped:
                     nc.vector.tensor_tensor(
                         out=sg[:].rearrange("p (t j) -> p t j", j=4),
-                        in0=r[:].rearrange("p (t j) -> p t j", j=4),
+                        in0=r[:].rearrange("p (j t) -> p t j", j=4),
                         in1=coeft[:, f, g * 4 : (g + 1) * 4].unsqueeze(1).to_broadcast([P, TOK, 4]),
                         op=ALU.mult,
                     )
@@ -221,10 +223,5 @@ def tile_efficient_skan_batch_kernel(tc, x, base_weight, grid, scale_sp, coef, c
             bank = psum.tile([P, 4, P], F32, tag="tp", bufs=2, name="bank")
             for t in range(TT):
                 nc.tensor.transpose(bank[:, t, :], y[:, t * P : (t + 1) * P], ident[:])
-            if ot % 2 == 0:
-                nc.scalar.copy(out=out_sb[:, :, ot * P : (ot + 1) * P], in_=bank[:])
-            else:
-                nc.vector.tensor_copy(out=out_sb[:, :, ot * P : (ot + 1) * P], in_=bank[:])
-            if ot % 3 == 2:
-                h = ot // 3
-                nc.sync.dma_start(out=out_view[:, :, h * 384 : (h + 1) * 384], in_=out_sb[:, :, h * 384 : (h + 1) * 384])
+            nc.scalar.copy(out=out_sb[:, :, ot * P : (ot + 1) * P], in_=bank[:])
+            nc.sync.dma_start(out=out_view[:, :, ot * P : (ot + 1) * P], in_=out_sb[:, :, ot * P : (ot + 1) * P])

@@ -22,11 +22,13 @@ OT = O // P
 TT = TOK // P
 G = K // 512
 CH = TOK * 4
+NC = NF * G
+LEAD = 2
 
 FLOPS = 2 * TOK * O * K * (NF + 1)
 
-GROUPED = (5, 13, 14, 15)
-VEC_EXIT_EVERY = 0
+GROUPED = ()
+PE_TURNED = (0, 1, 3, 4, 6, 7, 9, 10, 12, 13)
 
 
 def tile_efficient_skan_batch_kernel(tc, x, base_weight, grid, scale_sp, coef, conv_w, conv_b, out):
@@ -36,32 +38,38 @@ def tile_efficient_skan_batch_kernel(tc, x, base_weight, grid, scale_sp, coef, c
         work = ctx.enter_context(tc.tile_pool(name="work", bufs=2))
         psum = ctx.enter_context(tc.psum_pool(name="psum", bufs=1))
 
+        ident = const.tile([P, P], F32)
+        make_identity(nc, ident[:])
+        identb = const.tile([P, P], BF16)
+        make_identity(nc, identb[:])
+        ctx.enter_context(tc.manual_schedule())
+
         x_sb = const.tile([P, G, TT, K // G], BF16)
         x_view = x.rearrange("b (h p) (g k) -> p g (b h) k", p=P, g=G)
         for g in range(G):
             for h in range(2):
                 nc.sync.dma_start(out=x_sb[:, g, 2 * h : 2 * h + 2, :], in_=x_view[:, g, 2 * h : 2 * h + 2, :])
-
         grid_bc = const.tile([P, NF], BF16)
         nc.scalar.dma_start(out=grid_bc[:], in_=grid.partition_broadcast(P))
         coef_raw = const.tile([P, 4, 2 * NF], BF16)
         with nc.allow_non_contiguous_dma(reason="coef rows in runs of 32 bytes"):
             nc.scalar.dma_start(out=coef_raw[:], in_=coef.rearrange("(b p e) f -> p b (e f)", b=4, p=P, e=2))
         brow = const.tile([P, O], BF16)
-        nc.vector.memset(brow[:], 0.0)
-        nc.scalar.dma_start(out=brow[0:NF, :], in_=conv_b)
-        nc.scalar.dma_start(out=brow[NF : NF + 1, :], in_=scale_sp.rearrange("(a o) -> a o", a=1))
-
-        ident = const.tile([P, P], F32)
-        make_identity(nc, ident[:])
-        identb = const.tile([P, P], BF16)
-        make_identity(nc, identb[:])
+        nc.gpsimd.memset(brow[:], 0.0)
 
         def load_weights(m):
             w_raw = work.tile([P, OT, K], BF16, tag="w_raw", bufs=3, name="w_raw")
             src = base_weight if m == 0 else conv_w[m - 1]
-            nc.sync.dma_start(out=w_raw[:], in_=src.rearrange("(t p) k -> p t k", p=P))
+            for h in range(2):
+                ots = slice(3 * h, 3 * h + 3)
+                nc.sync.dma_start(out=w_raw[:, ots, :], in_=src.rearrange("(t p) k -> p t k", p=P)[:, ots, :])
             return w_raw
+
+        raws = [load_weights(0)]
+        nc.sync.dma_start(out=brow[0:NF, :], in_=conv_b)
+        nc.sync.dma_start(out=brow[NF : NF + 1, :], in_=scale_sp.rearrange("(a o) -> a o", a=1))
+        raws.append(load_weights(1))
+        raws.append(load_weights(2))
 
         g2 = const.tile([P, NF], F32)
         nc.vector.tensor_scalar(out=g2[:], in0=grid_bc[:], scalar1=1.0 / (2.0 * math.pi), scalar2=None, op0=ALU.mult)
@@ -80,138 +88,207 @@ def tile_efficient_skan_batch_kernel(tc, x, base_weight, grid, scale_sp, coef, c
                     nc.tensor.transpose(bank[:, t * P : (t + 1) * P], xw[:, g, u, t, :], ident[:])
                 dst = xp[:, (2 * g + u) * 1024 : (2 * g + u + 1) * 1024].rearrange("p (e t) -> p e t", e=2)
                 src = bank[:].bitcast(BF16).rearrange("p (t e) -> p e t", e=2)
-                if u == 0:
+                if g == 0 and u == 0:
                     nc.vector.tensor_copy(out=dst, in_=src)
                 else:
                     nc.scalar.copy(out=dst, in_=src)
 
-        bankb = psum.tile([P, OT, P], BF16, tag="tp", bufs=2, name="bankb")
-        for ot in range(OT):
-            nc.tensor.transpose(bankb[:, ot, :], brow[:, ot * P : (ot + 1) * P], identb[:])
-        bs = const.tile([P, OT, 16], F32)
-        nc.vector.tensor_copy(out=bs[:, :, 0 : NF + 1], in_=bankb[:, :, 0 : NF + 1])
-        cb = const.tile([P, OT], F32)
-        nc.vector.tensor_reduce(out=cb[:], in_=bs[:, :, 0:NF], axis=mybir.AxisListType.X, op=ALU.add)
-        scl = const.tile([P, OT], F32)
-        nc.vector.tensor_copy(out=scl[:], in_=bs[:, :, NF])
-        cbs = const.tile([P, OT], F32)
-        nc.vector.tensor_tensor(out=cbs[:], in0=cb[:], in1=scl[:], op=ALU.mult)
+        wgs, wqs = {}, {}
 
-        def weight_stage(m, w_raw):
-            ww = w_raw[:].rearrange("p t k -> p (t k)").bitcast(F32)
-            wg = work.tile([P, OT * 1024], BF16, tag="wg", bufs=2, name="wg", align_bytes=64)
-            wgw = wg[:].bitcast(F32)
-            wc = work.tile([P, OT * 256], U32, tag="wc", bufs=2, name="wc", align_bytes=64)
-            ws = work.tile([P, OT * 256], U8, tag="ws", bufs=2, name="ws", align_bytes=64)
-            for ot in range(OT):
+        def weight_exits(k):
+            m, h = k // 2, k % 2
+            if h == 0:
+                wc = work.tile([P, OT * 256], U32, tag="wc", bufs=3, name="wc", align_bytes=64)
+                ws = work.tile([P, OT * 256], U8, tag="ws", bufs=3, name="ws", align_bytes=64)
+                wqs[m] = (wc, ws)
+            ww = raws[m][:].rearrange("p t k -> p (t k)").bitcast(F32)
+            wg = work.tile([P, 3 * 1024], BF16, tag="wg", bufs=2, name="wg", align_bytes=64)
+            wgs[k] = wg
+            for i in range(3):
+                ot = 3 * h + i
                 bank = psum.tile([P, 4, P], F32, tag="tp", bufs=2, name="bank")
                 for b in range(4):
                     nc.tensor.transpose(bank[:, b, :], ww[:, ot * 512 + b * P : ot * 512 + (b + 1) * P], ident[:])
-                dst = wgw[:, ot * 512 : (ot + 1) * 512].rearrange("p (g o u) -> p g o u", g=G, o=P, u=2)
-                src = bank[:].rearrange("p (g u) o -> p g o u", g=G, u=2)
-                if VEC_EXIT_EVERY and (m * OT + ot) % VEC_EXIT_EVERY == 0:
-                    nc.vector.tensor_copy(out=dst, in_=src)
-                else:
-                    nc.scalar.copy(out=dst, in_=src)
-                if ot % 2 == 1:
-                    q = ot // 2
-                    nc.vector.quantize_mx(
-                        out=wc[:, q * 512 : (q + 1) * 512].bitcast(FP8X4),
-                        scales=ws[:, q * 512 : (q + 1) * 512],
-                        in_=wg[:, q * 2048 : (q + 1) * 2048],
-                    )
-            return wc, ws
+                nc.scalar.copy(
+                    out=wg[:].bitcast(F32)[:, i * 512 : (i + 1) * 512].rearrange("p (g o u) -> p g o u", g=G, o=P, u=2),
+                    in_=bank[:].rearrange("p (g u) o -> p g o u", g=G, u=2),
+                )
+
+        def weight_quantise(k):
+            m, h = k // 2, k % 2
+            wc, ws = wqs[m]
+            for a, b in ((0, 2), (2, 3)):
+                cols = slice((3 * h + a) * 256, (3 * h + b) * 256)
+                nc.vector.quantize_mx(
+                    out=wc[:, cols].bitcast(FP8X4), scales=ws[:, cols], in_=wgs[k][:, a * 1024 : b * 1024]
+                )
+
+        sas = {}
 
         def act_tiles():
             sc = work.tile([P, G * TOK], U32, tag="sc", bufs=3, name="sc", align_bytes=64)
             ss = work.tile([P, G * TOK], U8, tag="ss", bufs=3, name="ss", align_bytes=64)
             return sc, ss
 
-        def silu_stage():
-            sc, ss = act_tiles()
-            sl = const.tile([P, G * CH], BF16, align_bytes=64)
-            for g in range(G):
-                nc.scalar.activation(
-                    out=sl[:, g * CH : (g + 1) * CH].rearrange("p (c i j) -> p c j i", i=4, j=4),
-                    in_=xp[:, g * CH : (g + 1) * CH].rearrange("p (j c i) -> p c j i", j=4, i=4),
-                    func=ACT.Silu,
-                )
-            nc.vector.quantize_mx(out=sc[:].bitcast(FP8X4), scales=ss[:], in_=sl[:])
-            return sc, ss
+        ns, rs, sps, sgs = {}, {}, {}, {}
 
-        def sine_stage(f):
-            sc, ss = act_tiles()
-            gf = g2[:, f : f + 1]
-            for g in range(G):
-                grouped = (f * G + g) in GROUPED
-                xin = xp[:, g * CH : (g + 1) * CH]
-                n = work.tile([P, CH], I32, tag="n", bufs=2, name="n")
-                nc.vector.tensor_scalar(out=n[:], in0=xin, scalar1=gf, scalar2=None, op0=ALU.mult)
-                r = work.tile([P, CH], F32, tag="r", bufs=4, name="r")
-                nc.vector.scalar_tensor_tensor(out=r[:], in0=xin, scalar=gf, in1=n[:], op0=ALU.mult, op1=ALU.subtract)
-                nc.scalar.activation(out=r[:], in_=r[:], func=ACT.Sin, scale=2.0 * math.pi)
-                sg = work.tile([P, CH], BF16, tag="sg", bufs=2, name="sg", align_bytes=64)
-                if grouped:
-                    nc.vector.tensor_tensor(
-                        out=sg[:].rearrange("p (t j) -> p t j", j=4),
-                        in0=r[:].rearrange("p (j t) -> p t j", j=4),
-                        in1=coeft[:, f, g * 4 : (g + 1) * 4].unsqueeze(1).to_broadcast([P, TOK, 4]),
-                        op=ALU.mult,
-                    )
-                else:
-                    sp = work.tile([P, CH], BF16, tag="sp", bufs=2, name="sp")
-                    for j in range(4):
-                        nc.vector.tensor_scalar(
-                            out=sp[:, j * TOK : (j + 1) * TOK],
-                            in0=r[:, j * TOK : (j + 1) * TOK],
-                            scalar1=coeft[:, f, g * 4 + j : g * 4 + j + 1],
-                            scalar2=None,
-                            op0=ALU.mult,
+        def xin(c):
+            return xp[:, (c % G) * CH : (c % G + 1) * CH]
+
+        def periods(c):
+            ns[c] = work.tile([P, CH], I32, tag="n", bufs=2, name="n")
+            f = c // G
+            nc.vector.tensor_scalar(out=ns[c][:], in0=xin(c), scalar1=g2[:, f : f + 1], scalar2=None, op0=ALU.mult)
+
+        def reduce_range(c):
+            rs[c] = work.tile([P, CH], F32, tag="r", bufs=5, name="r")
+            f = c // G
+            nc.vector.scalar_tensor_tensor(
+                out=rs[c][:], in0=xin(c), scalar=g2[:, f : f + 1], in1=ns[c][:], op0=ALU.mult, op1=ALU.subtract
+            )
+
+        def sine(c):
+            nc.scalar.activation(out=rs[c][:], in_=rs[c][:], func=ACT.Sin, scale=2.0 * math.pi)
+
+        def times_coef(c):
+            f, g = c // G, c % G
+            if c in GROUPED:
+                sgs[c] = work.tile([P, CH], BF16, tag="sg", bufs=3, name="sg", align_bytes=64)
+                nc.vector.tensor_tensor(
+                    out=sgs[c][:].rearrange("p (t j) -> p t j", j=4),
+                    in0=rs[c][:].rearrange("p (j t) -> p t j", j=4),
+                    in1=coeft[:, f, g * 4 : (g + 1) * 4].unsqueeze(1).to_broadcast([P, TOK, 4]),
+                    op=ALU.mult,
+                )
+                return
+            sps[c] = work.tile([P, CH], BF16, tag="sp", bufs=2, name="sp")
+            for j in range(4):
+                cols = slice(j * TOK, (j + 1) * TOK)
+                nc.vector.tensor_scalar(
+                    out=sps[c][:, cols],
+                    in0=rs[c][:, cols],
+                    scalar1=coeft[:, f, g * 4 + j : g * 4 + j + 1],
+                    scalar2=None,
+                    op0=ALU.mult,
+                )
+
+        def turn(c):
+            if c in GROUPED:
+                return
+            sg = work.tile([P, CH], BF16, tag="sg", bufs=3, name="sg", align_bytes=64)
+            sgs[c] = sg
+            if c in PE_TURNED:
+                for h in range(2):
+                    bank = psum.tile([P, 2, P, 4], BF16, tag="tp", bufs=2, name="bank")
+                    for t in range(2):
+                        tok = (2 * h + t) * P
+                        nc.tensor.matmul(
+                            bank[:, t, :, :],
+                            lhsT=identb[:],
+                            rhs=sps[c][:].rearrange("p (j t) -> p t j", j=4)[:, tok : tok + P, :],
+                            start=True,
+                            stop=True,
                         )
-                    nc.scalar.copy(
-                        out=sg[:].rearrange("p (c i j) -> p c j i", i=4, j=4),
-                        in_=sp[:].rearrange("p (j c i) -> p c j i", j=4, i=4),
-                    )
-                nc.vector.quantize_mx(
-                    out=sc[:, g * TOK : (g + 1) * TOK].bitcast(FP8X4),
-                    scales=ss[:, g * TOK : (g + 1) * TOK],
-                    in_=sg[:],
+                    nc.scalar.copy(out=sg[:, h * 1024 : (h + 1) * 1024], in_=bank[:].rearrange("p a t j -> p (a t j)"))
+            else:
+                nc.scalar.copy(
+                    out=sg[:].rearrange("p (c i j) -> p c j i", i=4, j=4),
+                    in_=sps[c][:].rearrange("p (j c i) -> p c j i", j=4, i=4),
                 )
-            return sc, ss
 
-        def mx_stage(acc, wc, ws, sc, ss, first, last):
-            for g in range(G):
-                for ot in range(OT):
-                    cols = slice((ot * G + g) * P, (ot * G + g + 1) * P)
-                    nc.tensor.matmul_mx(
-                        out=acc[ot][:],
-                        lhsT=wc[:, cols].bitcast(FP8X4),
-                        lhsT_scale=ws[:, cols],
-                        rhs=sc[:, g * TOK : (g + 1) * TOK].bitcast(FP8X4),
-                        rhs_scale=ss[:, g * TOK : (g + 1) * TOK],
-                        start=(first and g == 0),
-                        stop=(last and g == G - 1),
-                    )
+        def quantise(c):
+            f, g = c // G, c % G
+            if g == 0:
+                sas[f] = act_tiles()
+            sc, ss = sas[f]
+            cols = slice(g * TOK, (g + 1) * TOK)
+            nc.vector.quantize_mx(out=sc[:, cols].bitcast(FP8X4), scales=ss[:, cols], in_=sgs[c][:])
+
+        def mx_pass(acc, w, sa, ot, g, start, stop):
+            cols = slice((ot * G + g) * P, (ot * G + g + 1) * P)
+            nc.tensor.matmul_mx(
+                out=acc[:],
+                lhsT=w[0][:, cols].bitcast(FP8X4),
+                lhsT_scale=w[1][:, cols],
+                rhs=sa[0][:, g * TOK : (g + 1) * TOK].bitcast(FP8X4),
+                rhs_scale=sa[1][:, g * TOK : (g + 1) * TOK],
+                start=start,
+                stop=stop,
+            )
 
         def new_acc():
             return [psum.tile([P, TOK], F32, tag="acc%d" % ot, bufs=1, name="acc%d" % ot) for ot in range(OT)]
 
-        raws = [load_weights(0), load_weights(1)]
-        wc, ws = weight_stage(0, raws[0])
-        sc, ss = silu_stage()
-        acc = new_acc()
-        mx_stage(acc, wc, ws, sc, ss, True, True)
+        sl = const.tile([P, G * CH], BF16, align_bytes=64)
+        for g in range(G):
+            nc.scalar.activation(
+                out=sl[:, g * CH : (g + 1) * CH].rearrange("p (c i j) -> p c j i", i=4, j=4),
+                in_=xp[:, g * CH : (g + 1) * CH].rearrange("p (j c i) -> p c j i", j=4, i=4),
+                func=ACT.Silu,
+            )
+        for c in range(LEAD):
+            periods(c)
+            reduce_range(c)
+        periods(LEAD)
+        weight_exits(0)
+        sa_base = act_tiles()
+        nc.vector.quantize_mx(out=sa_base[0][:].bitcast(FP8X4), scales=sa_base[1][:], in_=sl[:])
+        weight_quantise(0)
         base_c = const.tile([P, OT, TOK], F32)
-        for ot in range(OT):
-            nc.scalar.activation(out=base_c[:, ot, :], in_=acc[ot][:], func=ACT.Identity, bias=cbs[:, ot : ot + 1], scale=1.0)
+        scl = const.tile([P, OT], F32)
+        cbs = const.tile([P, OT], F32)
 
-        acc = new_acc()
-        for f in range(NF):
-            if f + 2 <= NF:
-                raws.append(load_weights(f + 2))
-            wc, ws = weight_stage(f + 1, raws[f + 1])
-            sc, ss = sine_stage(f)
-            mx_stage(acc, wc, ws, sc, ss, f == 0, f == NF - 1)
+        def bias_tables():
+            bankb = psum.tile([P, OT, P], BF16, tag="tp", bufs=2, name="bankb")
+            for ot in range(OT):
+                nc.tensor.transpose(bankb[:, ot, :], brow[:, ot * P : (ot + 1) * P], identb[:])
+            bs = const.tile([P, OT, 16], F32)
+            nc.vector.tensor_copy(out=bs[:, :, 0 : NF + 1], in_=bankb[:, :, 0 : NF + 1])
+            cb = const.tile([P, OT], F32)
+            nc.vector.tensor_reduce(out=cb[:], in_=bs[:, :, 0:NF], axis=mybir.AxisListType.X, op=ALU.add)
+            nc.vector.tensor_copy(out=scl[:], in_=bs[:, :, NF])
+            nc.vector.tensor_tensor(out=cbs[:], in0=cb[:], in1=scl[:], op=ALU.mult)
+
+        def base_exit(ot):
+            nc.scalar.activation(
+                out=base_c[:, ot, :], in_=acc[ot][:], func=ACT.Identity, bias=cbs[:, ot : ot + 1], scale=1.0
+            )
+
+        for s in range(NC + 3):
+            if s + 1 <= 2 * NF + 1:
+                if (s + 1) % 2 == 0 and (s + 1) // 2 + 2 <= NF:
+                    raws.append(load_weights((s + 1) // 2 + 2))
+                weight_exits(s + 1)
+            if s + LEAD < NC:
+                reduce_range(s + LEAD)
+            if 0 <= s - 3 < NC:
+                quantise(s - 3)
+            if 0 <= s - 2 < NC:
+                turn(s - 2)
+            if 0 <= s - 1 < NC:
+                times_coef(s - 1)
+            if s == 0:
+                bias_tables()
+            if s == 1:
+                acc = new_acc()
+                for ot in range(OT):
+                    for g in range(G):
+                        mx_pass(acc[ot], wqs[0], sa_base, ot, g, g == 0, g == G - 1)
+            if s in (1, 2):
+                for ot in range(3 * (s - 1), 3 * s):
+                    base_exit(ot)
+            if s < NC:
+                sine(s)
+            if s + LEAD + 1 < NC:
+                periods(s + LEAD + 1)
+            if s + 1 <= 2 * NF + 1:
+                weight_quantise(s + 1)
+            if s == 3:
+                acc = new_acc()
+            if s >= 3:
+                f, g = (s - 3) // G, (s - 3) % G
+                for ot in range(OT):
+                    mx_pass(acc[ot], wqs[f + 1], sas[f], ot, g, s == 3, s == NC + 2)
 
         out_sb = const.tile([P, TT, O], F32)
         out_view = out.rearrange("b (h p) o -> p (b h) o", p=P)

@@ -27,8 +27,8 @@ LEAD = 2
 
 FLOPS = 2 * TOK * O * K * (NF + 1)
 
-GROUPED = ()
-PE_TURNED = (0, 1, 3, 4, 6, 7, 9, 10, 12, 13)
+GROUPED = (2, 5, 8, 11, 14)
+PE_TURNED = ()
 
 
 def tile_efficient_skan_batch_kernel(tc, x, base_weight, grid, scale_sp, coef, conv_w, conv_b, out):

@@ -27,8 +27,7 @@ LEAD = 2
 
 FLOPS = 2 * TOK * O * K * (NF + 1)
 
-GROUPED = (2, 5, 8, 11, 14)
-PE_TURNED = ()
+GROUPED = (4, 9, 14, 15)
 
 
 def tile_efficient_skan_batch_kernel(tc, x, base_weight, grid, scale_sp, coef, conv_w, conv_b, out):
@@ -42,7 +41,6 @@ def tile_efficient_skan_batch_kernel(tc, x, base_weight, grid, scale_sp, coef, c
         make_identity(nc, ident[:])
         identb = const.tile([P, P], BF16)
         make_identity(nc, identb[:])
-        ctx.enter_context(tc.manual_schedule())
 
         x_sb = const.tile([P, G, TT, K // G], BF16)
         x_view = x.rearrange("b (h p) (g k) -> p g (b h) k", p=P, g=G)
@@ -70,6 +68,7 @@ def tile_efficient_skan_batch_kernel(tc, x, base_weight, grid, scale_sp, coef, c
         nc.sync.dma_start(out=brow[NF : NF + 1, :], in_=scale_sp.rearrange("(a o) -> a o", a=1))
         raws.append(load_weights(1))
         raws.append(load_weights(2))
+        raws.append(load_weights(3))
 
         g2 = const.tile([P, NF], F32)
         nc.vector.tensor_scalar(out=g2[:], in0=grid_bc[:], scalar1=1.0 / (2.0 * math.pi), scalar2=None, op0=ALU.mult)
@@ -88,7 +87,7 @@ def tile_efficient_skan_batch_kernel(tc, x, base_weight, grid, scale_sp, coef, c
                     nc.tensor.transpose(bank[:, t * P : (t + 1) * P], xw[:, g, u, t, :], ident[:])
                 dst = xp[:, (2 * g + u) * 1024 : (2 * g + u + 1) * 1024].rearrange("p (e t) -> p e t", e=2)
                 src = bank[:].bitcast(BF16).rearrange("p (t e) -> p e t", e=2)
-                if g == 0 and u == 0:
+                if u == 0:
                     nc.vector.tensor_copy(out=dst, in_=src)
                 else:
                     nc.scalar.copy(out=dst, in_=src)
@@ -98,8 +97,8 @@ def tile_efficient_skan_batch_kernel(tc, x, base_weight, grid, scale_sp, coef, c
         def weight_exits(k):
             m, h = k // 2, k % 2
             if h == 0:
-                wc = work.tile([P, OT * 256], U32, tag="wc", bufs=3, name="wc", align_bytes=64)
-                ws = work.tile([P, OT * 256], U8, tag="ws", bufs=3, name="ws", align_bytes=64)
+                wc = work.tile([P, OT * 256], U32, tag="wc", bufs=4, name="wc", align_bytes=64)
+                ws = work.tile([P, OT * 256], U8, tag="ws", bufs=4, name="ws", align_bytes=64)
                 wqs[m] = (wc, ws)
             ww = raws[m][:].rearrange("p t k -> p (t k)").bitcast(F32)
             wg = work.tile([P, 3 * 1024], BF16, tag="wg", bufs=2, name="wg", align_bytes=64)
@@ -147,19 +146,27 @@ def tile_efficient_skan_batch_kernel(tc, x, base_weight, grid, scale_sp, coef, c
                 out=rs[c][:], in0=xin(c), scalar=g2[:, f : f + 1], in1=ns[c][:], op0=ALU.mult, op1=ALU.subtract
             )
 
+        def tokens(c):
+            w = TOK // 2 if c == NC - 1 else TOK
+            return [slice(a, a + w) for a in range(0, TOK, w)]
+
         def sine(c):
-            nc.scalar.activation(out=rs[c][:], in_=rs[c][:], func=ACT.Sin, scale=2.0 * math.pi)
+            for ts in tokens(c):
+                part = rs[c][:].rearrange("p (j t) -> p j t", j=4)[:, :, ts]
+                nc.scalar.activation(out=part, in_=part, func=ACT.Sin, scale=2.0 * math.pi)
 
         def times_coef(c):
             f, g = c // G, c % G
             if c in GROUPED:
                 sgs[c] = work.tile([P, CH], BF16, tag="sg", bufs=3, name="sg", align_bytes=64)
-                nc.vector.tensor_tensor(
-                    out=sgs[c][:].rearrange("p (t j) -> p t j", j=4),
-                    in0=rs[c][:].rearrange("p (j t) -> p t j", j=4),
-                    in1=coeft[:, f, g * 4 : (g + 1) * 4].unsqueeze(1).to_broadcast([P, TOK, 4]),
-                    op=ALU.mult,
-                )
+                for ts in tokens(c):
+                    w = ts.stop - ts.start
+                    nc.vector.tensor_tensor(
+                        out=sgs[c][:, 4 * ts.start : 4 * ts.stop].rearrange("p (c i j) -> p c j i", i=4, j=4),
+                        in0=rs[c][:].rearrange("p (j t) -> p j t", j=4)[:, :, ts].rearrange("p j (c i) -> p c j i", i=4),
+                        in1=coeft[:, f, g * 4 : (g + 1) * 4].unsqueeze(1).unsqueeze(3).to_broadcast([P, w // 4, 4, 4]),
+                        op=ALU.mult,
+                    )
                 return
             sps[c] = work.tile([P, CH], BF16, tag="sp", bufs=2, name="sp")
             for j in range(4):
@@ -177,32 +184,21 @@ def tile_efficient_skan_batch_kernel(tc, x, base_weight, grid, scale_sp, coef, c
                 return
             sg = work.tile([P, CH], BF16, tag="sg", bufs=3, name="sg", align_bytes=64)
             sgs[c] = sg
-            if c in PE_TURNED:
-                for h in range(2):
-                    bank = psum.tile([P, 2, P, 4], BF16, tag="tp", bufs=2, name="bank")
-                    for t in range(2):
-                        tok = (2 * h + t) * P
-                        nc.tensor.matmul(
-                            bank[:, t, :, :],
-                            lhsT=identb[:],
-                            rhs=sps[c][:].rearrange("p (j t) -> p t j", j=4)[:, tok : tok + P, :],
-                            start=True,
-                            stop=True,
-                        )
-                    nc.scalar.copy(out=sg[:, h * 1024 : (h + 1) * 1024], in_=bank[:].rearrange("p a t j -> p (a t j)"))
-            else:
-                nc.scalar.copy(
-                    out=sg[:].rearrange("p (c i j) -> p c j i", i=4, j=4),
-                    in_=sps[c][:].rearrange("p (j c i) -> p c j i", j=4, i=4),
-                )
+            nc.scalar.copy(
+                out=sg[:].rearrange("p (c i j) -> p c j i", i=4, j=4),
+                in_=sps[c][:].rearrange("p (j c i) -> p c j i", j=4, i=4),
+            )
 
         def quantise(c):
             f, g = c // G, c % G
             if g == 0:
                 sas[f] = act_tiles()
             sc, ss = sas[f]
-            cols = slice(g * TOK, (g + 1) * TOK)
-            nc.vector.quantize_mx(out=sc[:, cols].bitcast(FP8X4), scales=ss[:, cols], in_=sgs[c][:])
+            for ts in tokens(c):
+                cols = slice(g * TOK + ts.start, g * TOK + ts.stop)
+                nc.vector.quantize_mx(
+                    out=sc[:, cols].bitcast(FP8X4), scales=ss[:, cols], in_=sgs[c][:, 4 * ts.start : 4 * ts.stop]
+                )
 
         def mx_pass(acc, w, sa, ot, g, start, stop):
             cols = slice((ot * G + g) * P, (ot * G + g + 1) * P)
@@ -234,6 +230,9 @@ def tile_efficient_skan_batch_kernel(tc, x, base_weight, grid, scale_sp, coef, c
         sa_base = act_tiles()
         nc.vector.quantize_mx(out=sa_base[0][:].bitcast(FP8X4), scales=sa_base[1][:], in_=sl[:])
         weight_quantise(0)
+        for k in (1, 2):
+            weight_exits(k)
+            weight_quantise(k)
         base_c = const.tile([P, OT, TOK], F32)
         scl = const.tile([P, OT], F32)
         cbs = const.tile([P, OT], F32)
@@ -255,10 +254,6 @@ def tile_efficient_skan_batch_kernel(tc, x, base_weight, grid, scale_sp, coef, c
             )
 
         for s in range(NC + 3):
-            if s + 1 <= 2 * NF + 1:
-                if (s + 1) % 2 == 0 and (s + 1) // 2 + 2 <= NF:
-                    raws.append(load_weights((s + 1) // 2 + 2))
-                weight_exits(s + 1)
             if s + LEAD < NC:
                 reduce_range(s + LEAD)
             if 0 <= s - 3 < NC:
@@ -281,8 +276,12 @@ def tile_efficient_skan_batch_kernel(tc, x, base_weight, grid, scale_sp, coef, c
                 sine(s)
             if s + LEAD + 1 < NC:
                 periods(s + LEAD + 1)
-            if s + 1 <= 2 * NF + 1:
-                weight_quantise(s + 1)
+            k = s + 3
+            if k <= 2 * NF + 1:
+                if k % 2 == 0 and k // 2 + 2 <= NF:
+                    raws.append(load_weights(k // 2 + 2))
+                weight_exits(k)
+                weight_quantise(k)
             if s == 3:
                 acc = new_acc()
             if s >= 3:

@@ -23,6 +23,7 @@ TT = TOK // P
 G = K // 512
 CH = TOK * 4
 NC = NF * G
+KEPT = 5
 LEAD = 2
 
 FLOPS = 2 * TOK * O * K * (NF + 1)
@@ -97,15 +98,17 @@ def tile_efficient_skan_batch_kernel(tc, x, base_weight, grid, scale_sp, coef, c
         def weight_exits(k):
             m, h = k // 2, k % 2
             if h == 0:
-                wc = work.tile([P, OT * 256], U32, tag="wc", bufs=4, name="wc", align_bytes=64)
-                ws = work.tile([P, OT * 256], U8, tag="ws", bufs=4, name="ws", align_bytes=64)
-                wqs[m] = (wc, ws)
+                wc = work.tile([P, KEPT * 256], U32, tag="wc", bufs=3, name="wc", align_bytes=64)
+                ws = work.tile([P, KEPT * 256], U8, tag="ws", bufs=3, name="ws", align_bytes=64)
+                lc = work.tile([P, 256], U32, tag="lc", bufs=NF, name="lc", align_bytes=64)
+                ls = work.tile([P, 256], U8, tag="ls", bufs=NF, name="ls", align_bytes=64)
+                wqs[m] = (wc, ws, lc, ls)
             ww = raws[m][:].rearrange("p t k -> p (t k)").bitcast(F32)
             wg = work.tile([P, 3 * 1024], BF16, tag="wg", bufs=2, name="wg", align_bytes=64)
             wgs[k] = wg
             for i in range(3):
                 ot = 3 * h + i
-                bank = psum.tile([P, 4, P], F32, tag="tp", bufs=2, name="bank")
+                bank = psum.tile([P, 4, P], F32, tag="tp", bufs=3, name="bank")
                 for b in range(4):
                     nc.tensor.transpose(bank[:, b, :], ww[:, ot * 512 + b * P : ot * 512 + (b + 1) * P], ident[:])
                 nc.scalar.copy(
@@ -115,18 +118,19 @@ def tile_efficient_skan_batch_kernel(tc, x, base_weight, grid, scale_sp, coef, c
 
         def weight_quantise(k):
             m, h = k // 2, k % 2
-            wc, ws = wqs[m]
+            wc, ws, lc, ls = wqs[m]
             for a, b in ((0, 2), (2, 3)):
                 cols = slice((3 * h + a) * 256, (3 * h + b) * 256)
+                codes, planes = (wc[:, cols], ws[:, cols]) if 3 * h + a < KEPT else (lc[:], ls[:])
                 nc.vector.quantize_mx(
-                    out=wc[:, cols].bitcast(FP8X4), scales=ws[:, cols], in_=wgs[k][:, a * 1024 : b * 1024]
+                    out=codes.bitcast(FP8X4), scales=planes, in_=wgs[k][:, a * 1024 : b * 1024]
                 )
 
         sas = {}
 
         def act_tiles():
-            sc = work.tile([P, G * TOK], U32, tag="sc", bufs=3, name="sc", align_bytes=64)
-            ss = work.tile([P, G * TOK], U8, tag="ss", bufs=3, name="ss", align_bytes=64)
+            sc = work.tile([P, G * TOK], U32, tag="sc", bufs=NF, name="sc", align_bytes=64)
+            ss = work.tile([P, G * TOK], U8, tag="ss", bufs=NF, name="ss", align_bytes=64)
             return sc, ss
 
         ns, rs, sps, sgs = {}, {}, {}, {}
@@ -140,7 +144,7 @@ def tile_efficient_skan_batch_kernel(tc, x, base_weight, grid, scale_sp, coef, c
             nc.vector.tensor_scalar(out=ns[c][:], in0=xin(c), scalar1=g2[:, f : f + 1], scalar2=None, op0=ALU.mult)
 
         def reduce_range(c):
-            rs[c] = work.tile([P, CH], F32, tag="r", bufs=5, name="r")
+            rs[c] = work.tile([P, CH], F32, tag="r", bufs=4, name="r")
             f = c // G
             nc.vector.scalar_tensor_tensor(
                 out=rs[c][:], in0=xin(c), scalar=g2[:, f : f + 1], in1=ns[c][:], op0=ALU.mult, op1=ALU.subtract
@@ -158,7 +162,7 @@ def tile_efficient_skan_batch_kernel(tc, x, base_weight, grid, scale_sp, coef, c
         def times_coef(c):
             f, g = c // G, c % G
             if c in GROUPED:
-                sgs[c] = work.tile([P, CH], BF16, tag="sg", bufs=3, name="sg", align_bytes=64)
+                sgs[c] = work.tile([P, CH], BF16, tag="sg", bufs=2, name="sg", align_bytes=64)
                 for ts in tokens(c):
                     w = ts.stop - ts.start
                     nc.vector.tensor_tensor(
@@ -182,7 +186,7 @@ def tile_efficient_skan_batch_kernel(tc, x, base_weight, grid, scale_sp, coef, c
         def turn(c):
             if c in GROUPED:
                 return
-            sg = work.tile([P, CH], BF16, tag="sg", bufs=3, name="sg", align_bytes=64)
+            sg = work.tile([P, CH], BF16, tag="sg", bufs=2, name="sg", align_bytes=64)
             sgs[c] = sg
             nc.scalar.copy(
                 out=sg[:].rearrange("p (c i j) -> p c j i", i=4, j=4),
@@ -201,19 +205,21 @@ def tile_efficient_skan_batch_kernel(tc, x, base_weight, grid, scale_sp, coef, c
                 )
 
         def mx_pass(acc, w, sa, ot, g, start, stop):
-            cols = slice((ot * G + g) * P, (ot * G + g + 1) * P)
+            codes, planes = (w[0], w[1]) if ot < KEPT else (w[2], w[3])
+            cols = slice((ot % KEPT * G + g) * P, (ot % KEPT * G + g + 1) * P)
             nc.tensor.matmul_mx(
                 out=acc[:],
-                lhsT=w[0][:, cols].bitcast(FP8X4),
-                lhsT_scale=w[1][:, cols],
+                lhsT=codes[:, cols].bitcast(FP8X4),
+                lhsT_scale=planes[:, cols],
                 rhs=sa[0][:, g * TOK : (g + 1) * TOK].bitcast(FP8X4),
                 rhs_scale=sa[1][:, g * TOK : (g + 1) * TOK],
                 start=start,
                 stop=stop,
             )
 
-        def new_acc():
-            return [psum.tile([P, TOK], F32, tag="acc%d" % ot, bufs=1, name="acc%d" % ot) for ot in range(OT)]
+        def new_acc(ot):
+            tag, bufs = ("acc%d" % ot, 1) if ot < KEPT else ("tp", 3)
+            return psum.tile([P, TOK], F32, tag=tag, bufs=bufs, name="acc%d" % ot)
 
         sl = const.tile([P, G * CH], BF16, align_bytes=64)
         for g in range(G):
@@ -238,7 +244,7 @@ def tile_efficient_skan_batch_kernel(tc, x, base_weight, grid, scale_sp, coef, c
         cbs = const.tile([P, OT], F32)
 
         def bias_tables():
-            bankb = psum.tile([P, OT, P], BF16, tag="tp", bufs=2, name="bankb")
+            bankb = psum.tile([P, OT, P], BF16, tag="tp", bufs=3, name="bankb")
             for ot in range(OT):
                 nc.tensor.transpose(bankb[:, ot, :], brow[:, ot * P : (ot + 1) * P], identb[:])
             bs = const.tile([P, OT, 16], F32)
@@ -265,7 +271,7 @@ def tile_efficient_skan_batch_kernel(tc, x, base_weight, grid, scale_sp, coef, c
             if s == 0:
                 bias_tables()
             if s == 1:
-                acc = new_acc()
+                acc = [new_acc(ot) for ot in range(OT)]
                 for ot in range(OT):
                     for g in range(G):
                         mx_pass(acc[ot], wqs[0], sa_base, ot, g, g == 0, g == G - 1)
@@ -283,20 +289,25 @@ def tile_efficient_skan_batch_kernel(tc, x, base_weight, grid, scale_sp, coef, c
                 weight_exits(k)
                 weight_quantise(k)
             if s == 3:
-                acc = new_acc()
+                acc = [new_acc(ot) for ot in range(KEPT)]
             if s >= 3:
                 f, g = (s - 3) // G, (s - 3) % G
-                for ot in range(OT):
+                for ot in range(KEPT):
                     mx_pass(acc[ot], wqs[f + 1], sas[f], ot, g, s == 3, s == NC + 2)
+            if s == NC:
+                acc.append(new_acc(KEPT))
+            if s >= NC:
+                for c in range(0 if s == NC else s - 3, s - 2):
+                    mx_pass(acc[KEPT], wqs[c // G + 1], sas[c // G], KEPT, c % G, c == 0, c == NC - 1)
 
         out_sb = const.tile([P, TT, O], F32)
         out_view = out.rearrange("b (h p) o -> p (b h) o", p=P)
         for ot in range(OT):
-            y = work.tile([P, TOK], F32, tag="y", bufs=3, name="y")
+            y = work.tile([P, TOK], F32, tag="y", bufs=2, name="y")
             nc.vector.scalar_tensor_tensor(
                 out=y[:], in0=acc[ot][:], scalar=scl[:, ot : ot + 1], in1=base_c[:, ot, :], op0=ALU.mult, op1=ALU.add
             )
-            bank = psum.tile([P, 4, P], F32, tag="tp", bufs=2, name="bank")
+            bank = psum.tile([P, 4, P], F32, tag="tp", bufs=3, name="bank")
             for t in range(TT):
                 nc.tensor.transpose(bank[:, t, :], y[:, t * P : (t + 1) * P], ident[:])
             nc.scalar.copy(out=out_sb[:, :, ot * P : (ot + 1) * P], in_=bank[:])

@@ -23,12 +23,13 @@ TT = TOK // P
 G = K // 512
 CH = TOK * 4
 NC = NF * G
-KEPT = 5
+KEPT = 4
 LEAD = 2
 
 FLOPS = 2 * TOK * O * K * (NF + 1)
 
-GROUPED = (4, 9, 14, 15)
+GROUPED = (3, 6, 8, 10, 12, 14, 15)
+HEAD = 2
 
 
 def tile_efficient_skan_batch_kernel(tc, x, base_weight, grid, scale_sp, coef, conv_w, conv_b, out):
@@ -38,10 +39,10 @@ def tile_efficient_skan_batch_kernel(tc, x, base_weight, grid, scale_sp, coef, c
         work = ctx.enter_context(tc.tile_pool(name="work", bufs=2))
         psum = ctx.enter_context(tc.psum_pool(name="psum", bufs=1))
 
-        ident = const.tile([P, P], F32)
-        make_identity(nc, ident[:])
         identb = const.tile([P, P], BF16)
         make_identity(nc, identb[:])
+        ident = const.tile([P, P], F32)
+        make_identity(nc, ident[:])
 
         x_sb = const.tile([P, G, TT, K // G], BF16)
         x_view = x.rearrange("b (h p) (g k) -> p g (b h) k", p=P, g=G)
@@ -79,19 +80,18 @@ def tile_efficient_skan_batch_kernel(tc, x, base_weight, grid, scale_sp, coef, c
             in_=coef_raw[:].rearrange("p b (e f) -> p f b e", e=2, f=NF),
         )
 
-        xw = x_sb[:].rearrange("p g t k -> p (g t k)").bitcast(F32).rearrange("p (g t u w) -> p g u t w", g=G, t=TT, u=2)
         xp = const.tile([P, G * CH], BF16, align_bytes=64)
         for g in range(G):
             for u in range(2):
-                bank = psum.tile([P, TOK], F32, tag="acc%d" % (2 * g + u), bufs=1, name="bank")
+                bank = psum.tile([P, 2, TOK], BF16, tag="acc%d" % (2 * g + u), bufs=1, name="bank")
                 for t in range(TT):
-                    nc.tensor.transpose(bank[:, t * P : (t + 1) * P], xw[:, g, u, t, :], ident[:])
-                dst = xp[:, (2 * g + u) * 1024 : (2 * g + u + 1) * 1024].rearrange("p (e t) -> p e t", e=2)
-                src = bank[:].bitcast(BF16).rearrange("p (t e) -> p e t", e=2)
-                if u == 0:
-                    nc.vector.tensor_copy(out=dst, in_=src)
-                else:
-                    nc.scalar.copy(out=dst, in_=src)
+                    for e in range(2):
+                        nc.tensor.transpose(
+                            bank[:, e, t * P : (t + 1) * P], x_sb[:, g, t, 256 * u + e : 256 * (u + 1) : 2], identb[:]
+                        )
+                nc.vector.tensor_copy(
+                    out=xp[:, (2 * g + u) * 1024 : (2 * g + u + 1) * 1024], in_=bank[:].rearrange("p e t -> p (e t)")
+                )
 
         wgs, wqs = {}, {}
 
@@ -100,15 +100,14 @@ def tile_efficient_skan_batch_kernel(tc, x, base_weight, grid, scale_sp, coef, c
             if h == 0:
                 wc = work.tile([P, KEPT * 256], U32, tag="wc", bufs=3, name="wc", align_bytes=64)
                 ws = work.tile([P, KEPT * 256], U8, tag="ws", bufs=3, name="ws", align_bytes=64)
-                lc = work.tile([P, 256], U32, tag="lc", bufs=NF, name="lc", align_bytes=64)
-                ls = work.tile([P, 256], U8, tag="ls", bufs=NF, name="ls", align_bytes=64)
+                lc = work.tile([P, (OT - KEPT) * 256], U32, tag="lc", bufs=NF, name="lc", align_bytes=64)
+                ls = work.tile([P, (OT - KEPT) * 256], U8, tag="ls", bufs=NF, name="ls", align_bytes=64)
                 wqs[m] = (wc, ws, lc, ls)
             ww = raws[m][:].rearrange("p t k -> p (t k)").bitcast(F32)
-            wg = work.tile([P, 3 * 1024], BF16, tag="wg", bufs=2, name="wg", align_bytes=64)
+            wg = work.tile([P, 4 * 1024], BF16, tag="wg", bufs=2, name="wg", align_bytes=64)
             wgs[k] = wg
-            for i in range(3):
-                ot = 3 * h + i
-                bank = psum.tile([P, 4, P], F32, tag="tp", bufs=3, name="bank")
+            for i, ot in enumerate(range(4) if h == 0 else range(4, OT)):
+                bank = psum.tile([P, 4, P], F32, tag="tp", bufs=2, name="bank")
                 for b in range(4):
                     nc.tensor.transpose(bank[:, b, :], ww[:, ot * 512 + b * P : ot * 512 + (b + 1) * P], ident[:])
                 nc.scalar.copy(
@@ -119,12 +118,8 @@ def tile_efficient_skan_batch_kernel(tc, x, base_weight, grid, scale_sp, coef, c
         def weight_quantise(k):
             m, h = k // 2, k % 2
             wc, ws, lc, ls = wqs[m]
-            for a, b in ((0, 2), (2, 3)):
-                cols = slice((3 * h + a) * 256, (3 * h + b) * 256)
-                codes, planes = (wc[:, cols], ws[:, cols]) if 3 * h + a < KEPT else (lc[:], ls[:])
-                nc.vector.quantize_mx(
-                    out=codes.bitcast(FP8X4), scales=planes, in_=wgs[k][:, a * 1024 : b * 1024]
-                )
+            codes, planes, width = (wc, ws, 4096) if h == 0 else (lc, ls, 2048)
+            nc.vector.quantize_mx(out=codes[:].bitcast(FP8X4), scales=planes[:], in_=wgs[k][:, 0:width])
 
         sas = {}
 
@@ -138,20 +133,47 @@ def tile_efficient_skan_batch_kernel(tc, x, base_weight, grid, scale_sp, coef, c
         def xin(c):
             return xp[:, (c % G) * CH : (c % G + 1) * CH]
 
+        xw = x_sb[:].rearrange("p g t k -> p (g t k)").bitcast(F32).rearrange("p (g t u w) -> p g u t w", g=G, t=TT, u=2)
+
+        def halves(c):
+            return [(u, slice((c % G * 2 + u) * 1024, (c % G * 2 + u + 1) * 1024)) for u in range(2)]
+
         def periods(c):
-            ns[c] = work.tile([P, CH], I32, tag="n", bufs=2, name="n")
             f = c // G
-            nc.vector.tensor_scalar(out=ns[c][:], in0=xin(c), scalar1=g2[:, f : f + 1], scalar2=None, op0=ALU.mult)
+            ns[c] = []
+            for u, cols in halves(c):
+                n = work.tile([P, 2, TOK], I32, tag="n", bufs=4, name="n")
+                xh = xp[:, cols].rearrange("p (e t) -> p e t", e=2)
+                if c < HEAD:
+                    nc.vector.tensor_scalar(out=n[:], in0=xh, scalar1=g2[:, f : f + 1], scalar2=None, op0=ALU.mult)
+                else:
+                    nc.gpsimd.tensor_scalar(
+                        out=n[:], in0=xh, scalar1=g2[:, f : f + 1], scalar2=0.0, op0=ALU.mult, op1=ALU.add
+                    )
+                ns[c].append(n)
 
         def reduce_range(c):
-            rs[c] = work.tile([P, CH], F32, tag="r", bufs=4, name="r")
-            f = c // G
-            nc.vector.scalar_tensor_tensor(
-                out=rs[c][:], in0=xin(c), scalar=g2[:, f : f + 1], in1=ns[c][:], op0=ALU.mult, op1=ALU.subtract
-            )
+            rs[c] = work.tile([P, CH], F32, tag="r", bufs=4, name="r", align_bytes=64)
+            f, g = c // G, c % G
+            for u, cols in halves(c):
+                if c < HEAD:
+                    xh = xp[:, cols].rearrange("p (e t) -> p e t", e=2)
+                else:
+                    bank = psum.tile([P, TOK], F32, tag="xb", bufs=2, name="bank")
+                    for t in range(TT):
+                        nc.tensor.transpose(bank[:, t * P : (t + 1) * P], xw[:, g, u, t, :], ident[:])
+                    xh = bank[:].bitcast(BF16).rearrange("p (t e) -> p e t", e=2)
+                nc.vector.scalar_tensor_tensor(
+                    out=rs[c][:, u * 1024 : (u + 1) * 1024].rearrange("p (e t) -> p e t", e=2),
+                    in0=xh,
+                    scalar=g2[:, f : f + 1],
+                    in1=ns[c][u][:],
+                    op0=ALU.mult,
+                    op1=ALU.subtract,
+                )
 
         def tokens(c):
-            w = TOK // 2 if c == NC - 1 else TOK
+            w = TOK // 4 if c == NC - 1 else TOK
             return [slice(a, a + w) for a in range(0, TOK, w)]
 
         def sine(c):
@@ -218,10 +240,10 @@ def tile_efficient_skan_batch_kernel(tc, x, base_weight, grid, scale_sp, coef, c
             )
 
         def new_acc(ot):
-            tag, bufs = ("acc%d" % ot, 1) if ot < KEPT else ("tp", 3)
+            tag, bufs = ("acc%d" % ot, 1) if ot < KEPT else ("xb", 2)
             return psum.tile([P, TOK], F32, tag=tag, bufs=bufs, name="acc%d" % ot)
 
-        sl = const.tile([P, G * CH], BF16, align_bytes=64)
+        sl = work.tile([P, G * CH], BF16, tag="r", bufs=4, name="sl", align_bytes=64)
         for g in range(G):
             nc.scalar.activation(
                 out=sl[:, g * CH : (g + 1) * CH].rearrange("p (c i j) -> p c j i", i=4, j=4),
@@ -244,7 +266,7 @@ def tile_efficient_skan_batch_kernel(tc, x, base_weight, grid, scale_sp, coef, c
         cbs = const.tile([P, OT], F32)
 
         def bias_tables():
-            bankb = psum.tile([P, OT, P], BF16, tag="tp", bufs=3, name="bankb")
+            bankb = psum.tile([P, OT, P], BF16, tag="tp", bufs=2, name="bankb")
             for ot in range(OT):
                 nc.tensor.transpose(bankb[:, ot, :], brow[:, ot * P : (ot + 1) * P], identb[:])
             bs = const.tile([P, OT, 16], F32)
@@ -295,19 +317,20 @@ def tile_efficient_skan_batch_kernel(tc, x, base_weight, grid, scale_sp, coef, c
                 for ot in range(KEPT):
                     mx_pass(acc[ot], wqs[f + 1], sas[f], ot, g, s == 3, s == NC + 2)
             if s == NC:
-                acc.append(new_acc(KEPT))
+                acc += [new_acc(ot) for ot in range(KEPT, OT)]
             if s >= NC:
-                for c in range(0 if s == NC else s - 3, s - 2):
-                    mx_pass(acc[KEPT], wqs[c // G + 1], sas[c // G], KEPT, c % G, c == 0, c == NC - 1)
+                for ot in range(KEPT, OT):
+                    for c in range(0 if s == NC else s - 3, s - 2):
+                        mx_pass(acc[ot], wqs[c // G + 1], sas[c // G], ot, c % G, c == 0, c == NC - 1)
 
-        out_sb = const.tile([P, TT, O], F32)
+        out_sb = work.tile([P, TT, O], F32, tag="w_raw", bufs=3, name="out_sb")
         out_view = out.rearrange("b (h p) o -> p (b h) o", p=P)
         for ot in range(OT):
             y = work.tile([P, TOK], F32, tag="y", bufs=2, name="y")
             nc.vector.scalar_tensor_tensor(
                 out=y[:], in0=acc[ot][:], scalar=scl[:, ot : ot + 1], in1=base_c[:, ot, :], op0=ALU.mult, op1=ALU.add
             )
-            bank = psum.tile([P, 4, P], F32, tag="tp", bufs=3, name="bank")
+            bank = psum.tile([P, 4, P], F32, tag="tp", bufs=2, name="bank")
             for t in range(TT):
                 nc.tensor.transpose(bank[:, t, :], y[:, t * P : (t + 1) * P], ident[:])
             nc.scalar.copy(out=out_sb[:, :, ot * P : (ot + 1) * P], in_=bank[:])

@@ -21,15 +21,20 @@ NF = 8
 OT = O // P
 TT = TOK // P
 G = K // 512
+HALF = K // G
+HCH = TOK * 2
 CH = TOK * 4
 NC = NF * G
-KEPT = 4
-LEAD = 2
+RUN = 4
+NRUN = NC // RUN
+NU = NC + G
+KEPT = 5
+WIDE = 4
 
 FLOPS = 2 * TOK * O * K * (NF + 1)
 
-GROUPED = (3, 6, 8, 10, 12, 14, 15)
-HEAD = 2
+ONE_PASS = (4, 2, 2, 2)
+TURN_PAIRS = (4, 3, 4, 0)
 
 
 def tile_efficient_skan_batch_kernel(tc, x, base_weight, grid, scale_sp, coef, conv_w, conv_b, out):
@@ -43,8 +48,12 @@ def tile_efficient_skan_batch_kernel(tc, x, base_weight, grid, scale_sp, coef, c
         make_identity(nc, identb[:])
         ident = const.tile([P, P], F32)
         make_identity(nc, ident[:])
+        warm = const.tile([P, 1], F32)
+        nc.scalar.activation(out=warm[:], in_=ident[:, 0:1], func=ACT.Silu)
+        brow = const.tile([P, O], BF16)
+        nc.gpsimd.memset(brow[:], 0.0)
 
-        x_sb = const.tile([P, G, TT, K // G], BF16)
+        x_sb = const.tile([P, G, TT, HALF], BF16)
         x_view = x.rearrange("b (h p) (g k) -> p g (b h) k", p=P, g=G)
         for g in range(G):
             for h in range(2):
@@ -54,23 +63,29 @@ def tile_efficient_skan_batch_kernel(tc, x, base_weight, grid, scale_sp, coef, c
         coef_raw = const.tile([P, 4, 2 * NF], BF16)
         with nc.allow_non_contiguous_dma(reason="coef rows in runs of 32 bytes"):
             nc.scalar.dma_start(out=coef_raw[:], in_=coef.rearrange("(b p e) f -> p b (e f)", b=4, p=P, e=2))
-        brow = const.tile([P, O], BF16)
-        nc.gpsimd.memset(brow[:], 0.0)
 
-        def load_weights(m):
-            w_raw = work.tile([P, OT, K], BF16, tag="w_raw", bufs=3, name="w_raw")
-            src = base_weight if m == 0 else conv_w[m - 1]
-            for h in range(2):
-                ots = slice(3 * h, 3 * h + 3)
-                nc.sync.dma_start(out=w_raw[:, ots, :], in_=src.rearrange("(t p) k -> p t k", p=P)[:, ots, :])
-            return w_raw
+        def where(c):
+            r = c // RUN
+            return r // 2 * RUN + c % RUN, (r + 1) // 2 % 2
 
-        raws = [load_weights(0)]
+        raws = {}
+
+        def load_weights(k):
+            raws[k] = work.tile([P, OT, HALF], BF16, tag="w_raw", bufs=4, name="w_raw")
+            if k < G:
+                src, g = base_weight, k
+            else:
+                f, g = where(k - G)
+                src = conv_w[f]
+            view = src.rearrange("(t p) k -> p t k", p=P)
+            nc.sync.dma_start(out=raws[k][:], in_=view[:, :, g * HALF : (g + 1) * HALF])
+
         nc.sync.dma_start(out=brow[0:NF, :], in_=conv_b)
         nc.sync.dma_start(out=brow[NF : NF + 1, :], in_=scale_sp.rearrange("(a o) -> a o", a=1))
-        raws.append(load_weights(1))
-        raws.append(load_weights(2))
-        raws.append(load_weights(3))
+        load_weights(0)
+        load_weights(1)
+        load_weights(2)
+        load_weights(3)
 
         g2 = const.tile([P, NF], F32)
         nc.vector.tensor_scalar(out=g2[:], in0=grid_bc[:], scalar1=1.0 / (2.0 * math.pi), scalar2=None, op0=ALU.mult)
@@ -79,126 +94,143 @@ def tile_efficient_skan_batch_kernel(tc, x, base_weight, grid, scale_sp, coef, c
             out=coeft[:].rearrange("p f (b e) -> p f b e", b=4, e=2),
             in_=coef_raw[:].rearrange("p b (e f) -> p f b e", e=2, f=NF),
         )
+        base_c = const.tile([P, OT, TOK], F32)
+        scl = const.tile([P, OT], F32)
+        cbs = const.tile([P, OT], F32)
+
+        ctx.enter_context(tc.manual_schedule())
 
         xp = const.tile([P, G * CH], BF16, align_bytes=64)
-        for g in range(G):
-            for u in range(2):
-                bank = psum.tile([P, 2, TOK], BF16, tag="acc%d" % (2 * g + u), bufs=1, name="bank")
-                for t in range(TT):
-                    for e in range(2):
-                        nc.tensor.transpose(
-                            bank[:, e, t * P : (t + 1) * P], x_sb[:, g, t, 256 * u + e : 256 * (u + 1) : 2], identb[:]
-                        )
-                nc.vector.tensor_copy(
-                    out=xp[:, (2 * g + u) * 1024 : (2 * g + u + 1) * 1024], in_=bank[:].rearrange("p e t -> p (e t)")
-                )
 
-        wgs, wqs = {}, {}
+        def x_bank(g, u, tag):
+            bank = psum.tile([P, 2, TOK], BF16, tag=tag, bufs=1, name="bank")
+            for t in range(TT):
+                for e in range(2):
+                    nc.tensor.transpose(
+                        bank[:, e, t * P : (t + 1) * P], x_sb[:, g, t, 256 * u + e : 256 * (u + 1) : 2], identb[:]
+                    )
+            return bank[:].rearrange("p e t -> p (e t)")
 
-        def weight_exits(k):
-            m, h = k // 2, k % 2
-            if h == 0:
-                wc = work.tile([P, KEPT * 256], U32, tag="wc", bufs=3, name="wc", align_bytes=64)
-                ws = work.tile([P, KEPT * 256], U8, tag="ws", bufs=3, name="ws", align_bytes=64)
-                lc = work.tile([P, (OT - KEPT) * 256], U32, tag="lc", bufs=NF, name="lc", align_bytes=64)
-                ls = work.tile([P, (OT - KEPT) * 256], U8, tag="ls", bufs=NF, name="ls", align_bytes=64)
-                wqs[m] = (wc, ws, lc, ls)
-            ww = raws[m][:].rearrange("p t k -> p (t k)").bitcast(F32)
-            wg = work.tile([P, 4 * 1024], BF16, tag="wg", bufs=2, name="wg", align_bytes=64)
-            wgs[k] = wg
-            for i, ot in enumerate(range(4) if h == 0 else range(4, OT)):
-                bank = psum.tile([P, 4, P], F32, tag="tp", bufs=2, name="bank")
-                for b in range(4):
-                    nc.tensor.transpose(bank[:, b, :], ww[:, ot * 512 + b * P : ot * 512 + (b + 1) * P], ident[:])
-                nc.scalar.copy(
-                    out=wg[:].bitcast(F32)[:, i * 512 : (i + 1) * 512].rearrange("p (g o u) -> p g o u", g=G, o=P, u=2),
-                    in_=bank[:].rearrange("p (g u) o -> p g o u", g=G, u=2),
-                )
+        def x_cols(g, u):
+            return xp[:, (2 * g + u) * HCH : (2 * g + u + 1) * HCH]
+
+        tps, wgs, wqs = {}, {}, {}
+
+        def weight_turn(k, i):
+            ww = raws[k][:].rearrange("p t k -> p (t k)").bitcast(F32)
+            bank = psum.tile([P, 4, P], F32, tag="tp", bufs=2, name="bank")
+            tps[k, i] = bank
+            for b in range(4):
+                nc.tensor.transpose(bank[:, b, :], ww[:, (4 * i + b) * P : (4 * i + b + 1) * P], ident[:])
+            if i == OT // 2 - 1 and k + 4 < NU:
+                load_weights(k + 4)
+
+        def weight_exit(k, i, on_vector):
+            if k not in wgs:
+                wgs[k] = work.tile([P, OT * HALF], BF16, tag="wg", bufs=4, name="wg", align_bytes=64)
+            dst = wgs[k][:, i * 1024 : (i + 1) * 1024].bitcast(F32).rearrange("p (t o u) -> p t o u", t=2, u=2)
+            src = tps[k, i][:].rearrange("p (t u) o -> p t o u", t=2, u=2)
+            if on_vector:
+                nc.vector.tensor_copy(out=dst, in_=src)
+            else:
+                nc.scalar.copy(out=dst, in_=src)
 
         def weight_quantise(k):
-            m, h = k // 2, k % 2
-            wc, ws, lc, ls = wqs[m]
-            codes, planes, width = (wc, ws, 4096) if h == 0 else (lc, ls, 2048)
-            nc.vector.quantize_mx(out=codes[:].bitcast(FP8X4), scales=planes[:], in_=wgs[k][:, 0:width])
+            wc = work.tile([P, WIDE * P], U32, tag="wc", bufs=6, name="wc", align_bytes=64)
+            ws = work.tile([P, WIDE * P], U8, tag="ws", bufs=6, name="ws", align_bytes=64)
+            lc = work.tile([P, (OT - WIDE) * P], U32, tag="lc", bufs=NC, name="lc", align_bytes=64)
+            ls = work.tile([P, (OT - WIDE) * P], U8, tag="ls", bufs=NC, name="ls", align_bytes=64)
+            wqs[k] = (wc, ws, lc, ls)
+            split = WIDE * HALF
+            nc.vector.quantize_mx(out=wc[:].bitcast(FP8X4), scales=ws[:], in_=wgs[k][:, 0:split])
+            nc.vector.quantize_mx(out=lc[:].bitcast(FP8X4), scales=ls[:], in_=wgs[k][:, split : OT * HALF])
 
         sas = {}
 
-        def act_tiles():
-            sc = work.tile([P, G * TOK], U32, tag="sc", bufs=NF, name="sc", align_bytes=64)
-            ss = work.tile([P, G * TOK], U8, tag="ss", bufs=NF, name="ss", align_bytes=64)
-            return sc, ss
+        def act_tiles(k):
+            sas[k] = (
+                work.tile([P, TOK], U32, tag="sc", bufs=NC, name="sc", align_bytes=64),
+                work.tile([P, TOK], U8, tag="ss", bufs=NC, name="ss", align_bytes=64),
+            )
 
         ns, rs, sps, sgs = {}, {}, {}, {}
 
-        def xin(c):
-            return xp[:, (c % G) * CH : (c % G + 1) * CH]
+        def place(h):
+            return h // (2 * RUN) * RUN + h % RUN, h // RUN % 2
 
-        xw = x_sb[:].rearrange("p g t k -> p (g t k)").bitcast(F32).rearrange("p (g t u w) -> p g u t w", g=G, t=TT, u=2)
-
-        def halves(c):
-            return [(u, slice((c % G * 2 + u) * 1024, (c % G * 2 + u + 1) * 1024)) for u in range(2)]
-
-        def periods(c):
-            f = c // G
-            ns[c] = []
-            for u, cols in halves(c):
-                n = work.tile([P, 2, TOK], I32, tag="n", bufs=4, name="n")
-                xh = xp[:, cols].rearrange("p (e t) -> p e t", e=2)
-                if c < HEAD:
-                    nc.vector.tensor_scalar(out=n[:], in0=xh, scalar1=g2[:, f : f + 1], scalar2=None, op0=ALU.mult)
-                else:
-                    nc.gpsimd.tensor_scalar(
-                        out=n[:], in0=xh, scalar1=g2[:, f : f + 1], scalar2=0.0, op0=ALU.mult, op1=ALU.add
-                    )
-                ns[c].append(n)
-
-        def reduce_range(c):
-            rs[c] = work.tile([P, CH], F32, tag="r", bufs=4, name="r", align_bytes=64)
-            f, g = c // G, c % G
-            for u, cols in halves(c):
-                if c < HEAD:
-                    xh = xp[:, cols].rearrange("p (e t) -> p e t", e=2)
-                else:
-                    bank = psum.tile([P, TOK], F32, tag="xb", bufs=2, name="bank")
-                    for t in range(TT):
-                        nc.tensor.transpose(bank[:, t * P : (t + 1) * P], xw[:, g, u, t, :], ident[:])
-                    xh = bank[:].bitcast(BF16).rearrange("p (t e) -> p e t", e=2)
-                nc.vector.scalar_tensor_tensor(
-                    out=rs[c][:, u * 1024 : (u + 1) * 1024].rearrange("p (e t) -> p e t", e=2),
-                    in0=xh,
-                    scalar=g2[:, f : f + 1],
-                    in1=ns[c][u][:],
-                    op0=ALU.mult,
-                    op1=ALU.subtract,
+        def periods(h, tick):
+            c, u = place(h)
+            f, g = where(c)
+            ns[h] = work.tile([P, HCH], I32, tag="n", bufs=3, name="n")
+            if h % RUN == 1 or h == 0:
+                nc.vector.tensor_scalar(
+                    out=ns[h][:], in0=x_cols(g, u), scalar1=g2[:, f : f + 1], scalar2=None, op0=ALU.mult
+                )
+            else:
+                nc.gpsimd.tensor_scalar(
+                    out=ns[h][:], in0=x_cols(g, u), scalar1=tick[:, f : f + 1], scalar2=0.0, op0=ALU.mult, op1=ALU.add
                 )
 
-        def tokens(c):
-            w = TOK // 4 if c == NC - 1 else TOK
-            return [slice(a, a + w) for a in range(0, TOK, w)]
+        emptied = [0]
 
-        def sine(c):
-            for ts in tokens(c):
-                part = rs[c][:].rearrange("p (j t) -> p j t", j=4)[:, :, ts]
+        def pair():
+            for i in range(emptied[0], min(emptied[0] + 2, 3 * NU)):
+                weight_turn(i // 3, i % 3)
+                weight_exit(i // 3, i % 3, False)
+                emptied[0] = i + 1
+
+        def weights_ready(most):
+            for k in range(len(wqs), min(len(wqs) + most, emptied[0] // 3)):
+                weight_quantise(k)
+
+        done = [0]
+
+        def multiply_ready(most):
+            for c in range(done[0], min(done[0] + most, NC)):
+                if G + c in wqs and G + c in sas:
+                    multiply(c)
+                    done[0] = c + 1
+
+        def stretch(b, xb, following, pairs):
+            tick = const.tile([P, NF], F32, name="tick%d" % b)
+            nc.vector.tensor_copy(out=tick[:], in_=g2[:])
+            for h in range(b * RUN, (b + 1) * RUN):
+                c, u = place(h)
+                f, g = where(c)
+                if u == 0:
+                    rs[c] = work.tile([P, CH], F32, tag="r", bufs=RUN, name="r", align_bytes=64)
+                part = rs[c][:, u * HCH : (u + 1) * HCH]
+                nc.vector.scalar_tensor_tensor(
+                    out=part, in0=xb, scalar=g2[:, f : f + 1], in1=ns[h][:], op0=ALU.mult, op1=ALU.subtract
+                )
+                if h + 2 < 2 * NC:
+                    periods(h + 2, tick)
                 nc.scalar.activation(out=part, in_=part, func=ACT.Sin, scale=2.0 * math.pi)
+                if h % RUN == RUN - 1 and following is not None:
+                    xbs.append(x_bank(following[0], following[1], "xb"))
+                if h % 2 == 1 and pairs:
+                    pair()
+                    if b > 3:
+                        multiply_ready(1)
 
-        def times_coef(c):
-            f, g = c // G, c % G
-            if c in GROUPED:
-                sgs[c] = work.tile([P, CH], BF16, tag="sg", bufs=2, name="sg", align_bytes=64)
-                for ts in tokens(c):
-                    w = ts.stop - ts.start
-                    nc.vector.tensor_tensor(
-                        out=sgs[c][:, 4 * ts.start : 4 * ts.stop].rearrange("p (c i j) -> p c j i", i=4, j=4),
-                        in0=rs[c][:].rearrange("p (j t) -> p j t", j=4)[:, :, ts].rearrange("p j (c i) -> p c j i", i=4),
-                        in1=coeft[:, f, g * 4 : (g + 1) * 4].unsqueeze(1).unsqueeze(3).to_broadcast([P, w // 4, 4, 4]),
-                        op=ALU.mult,
-                    )
+        def times_coef(c, a, b):
+            f, g = where(c)
+            if c % RUN >= RUN - ONE_PASS[c // RUN]:
+                if a == 0:
+                    sgs[c] = work.tile([P, CH], BF16, tag="sg", bufs=4, name="sg", align_bytes=64)
+                nc.vector.tensor_tensor(
+                    out=sgs[c][:, 4 * a : 4 * b].rearrange("p (c i j) -> p c j i", i=4, j=4),
+                    in0=rs[c][:].rearrange("p (j t) -> p j t", j=4)[:, :, a:b].rearrange("p j (c i) -> p c j i", i=4),
+                    in1=coeft[:, f, g * 4 : (g + 1) * 4].unsqueeze(1).unsqueeze(3).to_broadcast([P, (b - a) // 4, 4, 4]),
+                    op=ALU.mult,
+                )
                 return
-            sps[c] = work.tile([P, CH], BF16, tag="sp", bufs=2, name="sp")
+            sp = work.tile([P, CH], BF16, tag="sp", bufs=3, name="sp", align_bytes=64)
+            sps[c] = sp
             for j in range(4):
                 cols = slice(j * TOK, (j + 1) * TOK)
                 nc.vector.tensor_scalar(
-                    out=sps[c][:, cols],
+                    out=sp[:, cols],
                     in0=rs[c][:, cols],
                     scalar1=coeft[:, f, g * 4 + j : g * 4 + j + 1],
                     scalar2=None,
@@ -206,132 +238,162 @@ def tile_efficient_skan_batch_kernel(tc, x, base_weight, grid, scale_sp, coef, c
                 )
 
         def turn(c):
-            if c in GROUPED:
+            if c in sgs:
                 return
-            sg = work.tile([P, CH], BF16, tag="sg", bufs=2, name="sg", align_bytes=64)
+            sg = work.tile([P, CH], BF16, tag="sg", bufs=4, name="sg", align_bytes=64)
             sgs[c] = sg
             nc.scalar.copy(
-                out=sg[:].rearrange("p (c i j) -> p c j i", i=4, j=4),
-                in_=sps[c][:].rearrange("p (j c i) -> p c j i", j=4, i=4),
+                out=sg[:].rearrange("p (c i j) -> p c j i", i=8, j=4),
+                in_=sps[c][:].rearrange("p (j c i) -> p c j i", j=4, i=8),
             )
 
-        def quantise(c):
-            f, g = c // G, c % G
-            if g == 0:
-                sas[f] = act_tiles()
-            sc, ss = sas[f]
-            for ts in tokens(c):
-                cols = slice(g * TOK + ts.start, g * TOK + ts.stop)
-                nc.vector.quantize_mx(
-                    out=sc[:, cols].bitcast(FP8X4), scales=ss[:, cols], in_=sgs[c][:, 4 * ts.start : 4 * ts.stop]
-                )
+        def quantise(c, a, b):
+            if a == 0:
+                act_tiles(G + c)
+            sc, ss = sas[G + c]
+            nc.vector.quantize_mx(out=sc[:, a:b].bitcast(FP8X4), scales=ss[:, a:b], in_=sgs[c][:, 4 * a : 4 * b])
 
-        def mx_pass(acc, w, sa, ot, g, start, stop):
-            codes, planes = (w[0], w[1]) if ot < KEPT else (w[2], w[3])
-            cols = slice((ot % KEPT * G + g) * P, (ot % KEPT * G + g + 1) * P)
+        def mx_pass(acc, k, ot, start, stop):
+            w, sa = wqs[k], sas[k]
+            codes, planes = (w[0], w[1]) if ot < WIDE else (w[2], w[3])
+            cols = slice(ot % WIDE * P, (ot % WIDE + 1) * P)
             nc.tensor.matmul_mx(
                 out=acc[:],
                 lhsT=codes[:, cols].bitcast(FP8X4),
                 lhsT_scale=planes[:, cols],
-                rhs=sa[0][:, g * TOK : (g + 1) * TOK].bitcast(FP8X4),
-                rhs_scale=sa[1][:, g * TOK : (g + 1) * TOK],
+                rhs=sa[0][:].bitcast(FP8X4),
+                rhs_scale=sa[1][:],
                 start=start,
                 stop=stop,
             )
 
-        def new_acc(ot):
-            tag, bufs = ("acc%d" % ot, 1) if ot < KEPT else ("xb", 2)
-            return psum.tile([P, TOK], F32, tag=tag, bufs=bufs, name="acc%d" % ot)
+        def new_acc(tag):
+            return psum.tile([P, TOK], F32, tag=tag, bufs=1, name="acc")
 
-        sl = work.tile([P, G * CH], BF16, tag="r", bufs=4, name="sl", align_bytes=64)
-        for g in range(G):
+        accs, base_acc = {}, {}
+
+        def base_pass(ots):
+            for ot in ots:
+                base_acc[ot] = new_acc("acc%d" % (ot % KEPT))
+                for k in range(G):
+                    mx_pass(base_acc[ot], k, ot, k == 0, k == G - 1)
+
+        def base_exit(ots):
+            for ot in ots:
+                nc.scalar.activation(
+                    out=base_c[:, ot, :], in_=base_acc[ot][:], func=ACT.Identity, bias=cbs[:, ot : ot + 1], scale=1.0
+                )
+
+        def multiply(c):
+            for ot in range(KEPT):
+                if c == 0:
+                    accs[ot] = new_acc("acc%d" % ot)
+                mx_pass(accs[ot], G + c, ot, c == 0, c == NC - 1)
+
+        def multiply_last(cs):
+            for c in cs:
+                if c == 0:
+                    accs[OT - 1] = new_acc("xb")
+                mx_pass(accs[OT - 1], G + c, OT - 1, c == 0, c == NC - 1)
+
+        xb = x_bank(0, 0, "xb")
+        nc.vector.tensor_copy(out=x_cols(0, 0), in_=xb)
+        xb1 = x_bank(0, 1, "acc0")
+        nc.scalar.copy(out=x_cols(0, 1), in_=xb1)
+        late_x = [x_bank(1, u, "acc%d" % (1 + u)) for u in range(2)]
+        for h in range(2):
+            periods(h, None)
+        sls = [work.tile([P, CH], BF16, tag="sp", bufs=3, name="sl", align_bytes=64) for g in range(G)]
+
+        def base_silu(g):
             nc.scalar.activation(
-                out=sl[:, g * CH : (g + 1) * CH].rearrange("p (c i j) -> p c j i", i=4, j=4),
-                in_=xp[:, g * CH : (g + 1) * CH].rearrange("p (j c i) -> p c j i", j=4, i=4),
+                out=sls[g][:].rearrange("p (c i j) -> p c j i", i=8, j=4),
+                in_=xp[:, g * CH : (g + 1) * CH].rearrange("p (j c i) -> p c j i", j=4, i=8),
                 func=ACT.Silu,
             )
-        for c in range(LEAD):
-            periods(c)
-            reduce_range(c)
-        periods(LEAD)
-        weight_exits(0)
-        sa_base = act_tiles()
-        nc.vector.quantize_mx(out=sa_base[0][:].bitcast(FP8X4), scales=sa_base[1][:], in_=sl[:])
-        weight_quantise(0)
-        for k in (1, 2):
-            weight_exits(k)
-            weight_quantise(k)
-        base_c = const.tile([P, OT, TOK], F32)
-        scl = const.tile([P, OT], F32)
-        cbs = const.tile([P, OT], F32)
 
-        def bias_tables():
-            bankb = psum.tile([P, OT, P], BF16, tag="tp", bufs=2, name="bankb")
-            for ot in range(OT):
-                nc.tensor.transpose(bankb[:, ot, :], brow[:, ot * P : (ot + 1) * P], identb[:])
-            bs = const.tile([P, OT, 16], F32)
-            nc.vector.tensor_copy(out=bs[:, :, 0 : NF + 1], in_=bankb[:, :, 0 : NF + 1])
-            cb = const.tile([P, OT], F32)
-            nc.vector.tensor_reduce(out=cb[:], in_=bs[:, :, 0:NF], axis=mybir.AxisListType.X, op=ALU.add)
-            nc.vector.tensor_copy(out=scl[:], in_=bs[:, :, NF])
-            nc.vector.tensor_tensor(out=cbs[:], in0=cb[:], in1=scl[:], op=ALU.mult)
+        base_silu(0)
+        xbs = []
+        stretch(0, xb, (1, 0), False)
+        for u in range(2):
+            nc.scalar.copy(out=x_cols(1, u), in_=late_x[u])
+        bankb = psum.tile([P, OT, P], BF16, tag="acc3", bufs=1, name="bankb")
+        for ot in range(OT):
+            nc.tensor.transpose(bankb[:, ot, :], brow[:, ot * P : (ot + 1) * P], identb[:])
+        stretch(1, xb1, None, False)
+        base_silu(1)
+        cb = const.tile([P, OT], F32)
+        nc.vector.tensor_reduce(out=cb[:], in_=bankb[:, :, 0:NF], axis=mybir.AxisListType.X, op=ALU.add)
+        nc.vector.tensor_copy(out=scl[:], in_=bankb[:, :, NF])
+        for c in range(RUN):
+            times_coef(c, 0, TOK)
+            turn(c)
+            if c == 2:
+                nc.vector.tensor_tensor(out=cbs[:], in0=cb[:], in1=scl[:], op=ALU.mult)
+                weights_ready(1)
+                for g in range(G):
+                    act_tiles(g)
+                    nc.vector.quantize_mx(out=sas[g][0][:].bitcast(FP8X4), scales=sas[g][1][:], in_=sls[g][:])
+            pair()
+            pair()
+        weights_ready(2)
+        base_pass(range(KEPT))
+        base_exit(range(2))
+        base_pass(range(KEPT, OT))
 
-        def base_exit(ot):
-            nc.scalar.activation(
-                out=base_c[:, ot, :], in_=acc[ot][:], func=ACT.Identity, bias=cbs[:, ot : ot + 1], scale=1.0
-            )
+        for r in range(1, NRUN):
+            stretch(2 * r, xbs[-1], (where(r * RUN)[1], 1), True)
+            if r == 1:
+                base_exit(range(2, OT))
+            for c in range((r - 1) * RUN, r * RUN):
+                quantise(c, 0, TOK)
+            weights_ready(2)
+            if r > 1:
+                multiply_ready(2)
+            stretch(2 * r + 1, xbs[-1], (where((r + 1) * RUN)[1], 0) if r < NRUN - 1 else None, True)
+            if r == NRUN - 1:
+                break
+            for c in range(r * RUN, (r + 1) * RUN):
+                times_coef(c, 0, TOK)
+                turn(c)
+                if c % RUN < TURN_PAIRS[r]:
+                    pair()
+                multiply_ready(1)
+                if c % RUN >= 1:
+                    weights_ready(1)
 
-        for s in range(NC + 3):
-            if s + LEAD < NC:
-                reduce_range(s + LEAD)
-            if 0 <= s - 3 < NC:
-                quantise(s - 3)
-            if 0 <= s - 2 < NC:
-                turn(s - 2)
-            if 0 <= s - 1 < NC:
-                times_coef(s - 1)
-            if s == 0:
-                bias_tables()
-            if s == 1:
-                acc = [new_acc(ot) for ot in range(OT)]
-                for ot in range(OT):
-                    for g in range(G):
-                        mx_pass(acc[ot], wqs[0], sa_base, ot, g, g == 0, g == G - 1)
-            if s in (1, 2):
-                for ot in range(3 * (s - 1), 3 * s):
-                    base_exit(ot)
-            if s < NC:
-                sine(s)
-            if s + LEAD + 1 < NC:
-                periods(s + LEAD + 1)
-            k = s + 3
-            if k <= 2 * NF + 1:
-                if k % 2 == 0 and k // 2 + 2 <= NF:
-                    raws.append(load_weights(k // 2 + 2))
-                weight_exits(k)
-                weight_quantise(k)
-            if s == 3:
-                acc = [new_acc(ot) for ot in range(KEPT)]
-            if s >= 3:
-                f, g = (s - 3) // G, (s - 3) % G
-                for ot in range(KEPT):
-                    mx_pass(acc[ot], wqs[f + 1], sas[f], ot, g, s == 3, s == NC + 2)
-            if s == NC:
-                acc += [new_acc(ot) for ot in range(KEPT, OT)]
-            if s >= NC:
-                for ot in range(KEPT, OT):
-                    for c in range(0 if s == NC else s - 3, s - 2):
-                        mx_pass(acc[ot], wqs[c // G + 1], sas[c // G], ot, c % G, c == 0, c == NC - 1)
+        last = NC - RUN
+        multiply_ready(RUN)
+        multiply_last(range(last))
+        for c in range(last, NC - 1):
+            times_coef(c, 0, TOK)
+            turn(c)
+        weights_ready(2)
+        for c in (last, NC - 2, last + 1):
+            quantise(c, 0, TOK)
+            multiply(c)
+            multiply_last([c])
+            weights_ready(1)
+        step = TOK // 4
+        for a in range(0, TOK + step, step):
+            if a < TOK:
+                times_coef(NC - 1, a, a + step)
+            if a > 0:
+                quantise(NC - 1, a - step, a)
+        multiply(NC - 1)
+        multiply_last([NC - 1])
 
-        out_sb = work.tile([P, TT, O], F32, tag="w_raw", bufs=3, name="out_sb")
         out_view = out.rearrange("b (h p) o -> p (b h) o", p=P)
         for ot in range(OT):
             y = work.tile([P, TOK], F32, tag="y", bufs=2, name="y")
             nc.vector.scalar_tensor_tensor(
-                out=y[:], in0=acc[ot][:], scalar=scl[:, ot : ot + 1], in1=base_c[:, ot, :], op0=ALU.mult, op1=ALU.add
+                out=y[:], in0=accs[ot][:], scalar=scl[:, ot : ot + 1], in1=base_c[:, ot, :], op0=ALU.mult, op1=ALU.add
             )
             bank = psum.tile([P, 4, P], F32, tag="tp", bufs=2, name="bank")
             for t in range(TT):
                 nc.tensor.transpose(bank[:, t, :], y[:, t * P : (t + 1) * P], ident[:])
-            nc.scalar.copy(out=out_sb[:, :, ot * P : (ot + 1) * P], in_=bank[:])
-            nc.sync.dma_start(out=out_view[:, :, ot * P : (ot + 1) * P], in_=out_sb[:, :, ot * P : (ot + 1) * P])
+            if ot % 2 == 0:
+                osb = work.tile([P, TT, 2 * P], F32, tag="sg", bufs=4, name="osb", align_bytes=64)
+            nc.scalar.copy(out=osb[:, :, ot % 2 * P : (ot % 2 + 1) * P], in_=bank[:])
+            if ot % 2 == 1:
+                nc.sync.dma_start(out=out_view[:, :, (ot - 1) * P : (ot + 1) * P], in_=osb[:])

import math
from contextlib import ExitStack

import concourse.mybir as mybir
from concourse.masks import make_identity

F32 = mybir.dt.float32
BF16 = mybir.dt.bfloat16
I32 = mybir.dt.int32
U32 = mybir.dt.uint32
U8 = mybir.dt.uint8
FP8X4 = mybir.dt.float8_e4m3fn_x4
ALU = mybir.AluOpType
ACT = mybir.ActivationFunctionType

P = 128
TOK = 512
K = 1024
O = 768
NF = 8
OT = O // P
TT = TOK // P
G = K // 512
HALF = K // G
HCH = TOK * 2
CH = TOK * 4
NC = NF * G
RUN = 4
NRUN = NC // RUN
NU = NC + G
KEPT = 5
WIDE = 4

FLOPS = 2 * TOK * O * K * (NF + 1)

ONE_PASS = (4, 2, 2, 2)
TURN_PAIRS = (4, 3, 4, 0)


def tile_efficient_skan_batch_kernel(tc, x, base_weight, grid, scale_sp, coef, conv_w, conv_b, out):
    nc = tc.nc
    with ExitStack() as ctx:
        const = ctx.enter_context(tc.tile_pool(name="const", bufs=1))
        work = ctx.enter_context(tc.tile_pool(name="work", bufs=2))
        psum = ctx.enter_context(tc.psum_pool(name="psum", bufs=1))

        identb = const.tile([P, P], BF16)
        make_identity(nc, identb[:])
        ident = const.tile([P, P], F32)
        make_identity(nc, ident[:])
        warm = const.tile([P, 1], F32)
        nc.scalar.activation(out=warm[:], in_=ident[:, 0:1], func=ACT.Silu)
        brow = const.tile([P, O], BF16)
        nc.gpsimd.memset(brow[:], 0.0)

        x_sb = const.tile([P, G, TT, HALF], BF16)
        x_view = x.rearrange("b (h p) (g k) -> p g (b h) k", p=P, g=G)
        for g in range(G):
            for h in range(2):
                nc.sync.dma_start(out=x_sb[:, g, 2 * h : 2 * h + 2, :], in_=x_view[:, g, 2 * h : 2 * h + 2, :])
        grid_bc = const.tile([P, NF], BF16)
        nc.scalar.dma_start(out=grid_bc[:], in_=grid.partition_broadcast(P))
        coef_raw = const.tile([P, 4, 2 * NF], BF16)
        with nc.allow_non_contiguous_dma(reason="coef rows in runs of 32 bytes"):
            nc.scalar.dma_start(out=coef_raw[:], in_=coef.rearrange("(b p e) f -> p b (e f)", b=4, p=P, e=2))

        def where(c):
            r = c // RUN
            return r // 2 * RUN + c % RUN, (r + 1) // 2 % 2

        raws = {}

        def load_weights(k):
            raws[k] = work.tile([P, OT, HALF], BF16, tag="w_raw", bufs=4, name="w_raw")
            if k < G:
                src, g = base_weight, k
            else:
                f, g = where(k - G)
                src = conv_w[f]
            view = src.rearrange("(t p) k -> p t k", p=P)
            nc.sync.dma_start(out=raws[k][:], in_=view[:, :, g * HALF : (g + 1) * HALF])

        nc.sync.dma_start(out=brow[0:NF, :], in_=conv_b)
        nc.sync.dma_start(out=brow[NF : NF + 1, :], in_=scale_sp.rearrange("(a o) -> a o", a=1))
        load_weights(0)
        load_weights(1)
        load_weights(2)
        load_weights(3)

        g2 = const.tile([P, NF], F32)
        nc.vector.tensor_scalar(out=g2[:], in0=grid_bc[:], scalar1=1.0 / (2.0 * math.pi), scalar2=None, op0=ALU.mult)
        coeft = const.tile([P, NF, 8], F32)
        nc.vector.tensor_copy(
            out=coeft[:].rearrange("p f (b e) -> p f b e", b=4, e=2),
            in_=coef_raw[:].rearrange("p b (e f) -> p f b e", e=2, f=NF),
        )
        base_c = const.tile([P, OT, TOK], F32)
        scl = const.tile([P, OT], F32)
        cbs = const.tile([P, OT], F32)

        ctx.enter_context(tc.manual_schedule())

        xp = const.tile([P, G * CH], BF16, align_bytes=64)

        def x_bank(g, u, tag):
            bank = psum.tile([P, 2, TOK], BF16, tag=tag, bufs=1, name="bank")
            for t in range(TT):
                for e in range(2):
                    nc.tensor.transpose(
                        bank[:, e, t * P : (t + 1) * P], x_sb[:, g, t, 256 * u + e : 256 * (u + 1) : 2], identb[:]
                    )
            return bank[:].rearrange("p e t -> p (e t)")

        def x_cols(g, u):
            return xp[:, (2 * g + u) * HCH : (2 * g + u + 1) * HCH]

        tps, wgs, wqs = {}, {}, {}

        def weight_turn(k, i):
            ww = raws[k][:].rearrange("p t k -> p (t k)").bitcast(F32)
            bank = psum.tile([P, 4, P], F32, tag="tp", bufs=2, name="bank")
            tps[k, i] = bank
            for b in range(4):
                nc.tensor.transpose(bank[:, b, :], ww[:, (4 * i + b) * P : (4 * i + b + 1) * P], ident[:])
            if i == OT // 2 - 1 and k + 4 < NU:
                load_weights(k + 4)

        def weight_exit(k, i, on_vector):
            if k not in wgs:
                wgs[k] = work.tile([P, OT * HALF], BF16, tag="wg", bufs=4, name="wg", align_bytes=64)
            dst = wgs[k][:, i * 1024 : (i + 1) * 1024].bitcast(F32).rearrange("p (t o u) -> p t o u", t=2, u=2)
            src = tps[k, i][:].rearrange("p (t u) o -> p t o u", t=2, u=2)
            if on_vector:
                nc.vector.tensor_copy(out=dst, in_=src)
            else:
                nc.scalar.copy(out=dst, in_=src)

        def weight_quantise(k):
            wc = work.tile([P, WIDE * P], U32, tag="wc", bufs=6, name="wc", align_bytes=64)
            ws = work.tile([P, WIDE * P], U8, tag="ws", bufs=6, name="ws", align_bytes=64)
            lc = work.tile([P, (OT - WIDE) * P], U32, tag="lc", bufs=NC, name="lc", align_bytes=64)
            ls = work.tile([P, (OT - WIDE) * P], U8, tag="ls", bufs=NC, name="ls", align_bytes=64)
            wqs[k] = (wc, ws, lc, ls)
            split = WIDE * HALF
            nc.vector.quantize_mx(out=wc[:].bitcast(FP8X4), scales=ws[:], in_=wgs[k][:, 0:split])
            nc.vector.quantize_mx(out=lc[:].bitcast(FP8X4), scales=ls[:], in_=wgs[k][:, split : OT * HALF])

        sas = {}

        def act_tiles(k):
            sas[k] = (
                work.tile([P, TOK], U32, tag="sc", bufs=NC, name="sc", align_bytes=64),
                work.tile([P, TOK], U8, tag="ss", bufs=NC, name="ss", align_bytes=64),
            )

        ns, rs, sps, sgs = {}, {}, {}, {}

        def place(h):
            return h // (2 * RUN) * RUN + h % RUN, h // RUN % 2

        def periods(h, tick):
            c, u = place(h)
            f, g = where(c)
            ns[h] = work.tile([P, HCH], I32, tag="n", bufs=3, name="n")
            if h % RUN == 1 or h == 0:
                nc.vector.tensor_scalar(
                    out=ns[h][:], in0=x_cols(g, u), scalar1=g2[:, f : f + 1], scalar2=None, op0=ALU.mult
                )
            else:
                nc.gpsimd.tensor_scalar(
                    out=ns[h][:], in0=x_cols(g, u), scalar1=tick[:, f : f + 1], scalar2=0.0, op0=ALU.mult, op1=ALU.add
                )

        emptied = [0]

        def pair():
            for i in range(emptied[0], min(emptied[0] + 2, 3 * NU)):
                weight_turn(i // 3, i % 3)
                weight_exit(i // 3, i % 3, False)
                emptied[0] = i + 1

        def weights_ready(most):
            for k in range(len(wqs), min(len(wqs) + most, emptied[0] // 3)):
                weight_quantise(k)

        done = [0]

        def multiply_ready(most):
            for c in range(done[0], min(done[0] + most, NC)):
                if G + c in wqs and G + c in sas:
                    multiply(c)
                    done[0] = c + 1

        def stretch(b, xb, following, pairs):
            tick = const.tile([P, NF], F32, name="tick%d" % b)
            nc.vector.tensor_copy(out=tick[:], in_=g2[:])
            for h in range(b * RUN, (b + 1) * RUN):
                c, u = place(h)
                f, g = where(c)
                if u == 0:
                    rs[c] = work.tile([P, CH], F32, tag="r", bufs=RUN, name="r", align_bytes=64)
                part = rs[c][:, u * HCH : (u + 1) * HCH]
                nc.vector.scalar_tensor_tensor(
                    out=part, in0=xb, scalar=g2[:, f : f + 1], in1=ns[h][:], op0=ALU.mult, op1=ALU.subtract
                )
                if h + 2 < 2 * NC:
                    periods(h + 2, tick)
                nc.scalar.activation(out=part, in_=part, func=ACT.Sin, scale=2.0 * math.pi)
                if h % RUN == RUN - 1 and following is not None:
                    xbs.append(x_bank(following[0], following[1], "xb"))
                if h % 2 == 1 and pairs:
                    pair()
                    if b > 3:
                        multiply_ready(1)

        def times_coef(c, a, b):
            f, g = where(c)
            if c % RUN >= RUN - ONE_PASS[c // RUN]:
                if a == 0:
                    sgs[c] = work.tile([P, CH], BF16, tag="sg", bufs=4, name="sg", align_bytes=64)
                nc.vector.tensor_tensor(
                    out=sgs[c][:, 4 * a : 4 * b].rearrange("p (c i j) -> p c j i", i=4, j=4),
                    in0=rs[c][:].rearrange("p (j t) -> p j t", j=4)[:, :, a:b].rearrange("p j (c i) -> p c j i", i=4),
                    in1=coeft[:, f, g * 4 : (g + 1) * 4].unsqueeze(1).unsqueeze(3).to_broadcast([P, (b - a) // 4, 4, 4]),
                    op=ALU.mult,
                )
                return
            sp = work.tile([P, CH], BF16, tag="sp", bufs=3, name="sp", align_bytes=64)
            sps[c] = sp
            for j in range(4):
                cols = slice(j * TOK, (j + 1) * TOK)
                nc.vector.tensor_scalar(
                    out=sp[:, cols],
                    in0=rs[c][:, cols],
                    scalar1=coeft[:, f, g * 4 + j : g * 4 + j + 1],
                    scalar2=None,
                    op0=ALU.mult,
                )

        def turn(c):
            if c in sgs:
                return
            sg = work.tile([P, CH], BF16, tag="sg", bufs=4, name="sg", align_bytes=64)
            sgs[c] = sg
            nc.scalar.copy(
                out=sg[:].rearrange("p (c i j) -> p c j i", i=8, j=4),
                in_=sps[c][:].rearrange("p (j c i) -> p c j i", j=4, i=8),
            )

        def quantise(c, a, b):
            if a == 0:
                act_tiles(G + c)
            sc, ss = sas[G + c]
            nc.vector.quantize_mx(out=sc[:, a:b].bitcast(FP8X4), scales=ss[:, a:b], in_=sgs[c][:, 4 * a : 4 * b])

        def mx_pass(acc, k, ot, start, stop):
            w, sa = wqs[k], sas[k]
            codes, planes = (w[0], w[1]) if ot < WIDE else (w[2], w[3])
            cols = slice(ot % WIDE * P, (ot % WIDE + 1) * P)
            nc.tensor.matmul_mx(
                out=acc[:],
                lhsT=codes[:, cols].bitcast(FP8X4),
                lhsT_scale=planes[:, cols],
                rhs=sa[0][:].bitcast(FP8X4),
                rhs_scale=sa[1][:],
                start=start,
                stop=stop,
            )

        def new_acc(tag):
            return psum.tile([P, TOK], F32, tag=tag, bufs=1, name="acc")

        accs, base_acc = {}, {}

        def base_pass(ots):
            for ot in ots:
                base_acc[ot] = new_acc("acc%d" % (ot % KEPT))
                for k in range(G):
                    mx_pass(base_acc[ot], k, ot, k == 0, k == G - 1)

        def base_exit(ots):
            for ot in ots:
                nc.scalar.activation(
                    out=base_c[:, ot, :], in_=base_acc[ot][:], func=ACT.Identity, bias=cbs[:, ot : ot + 1], scale=1.0
                )

        def multiply(c):
            for ot in range(KEPT):
                if c == 0:
                    accs[ot] = new_acc("acc%d" % ot)
                mx_pass(accs[ot], G + c, ot, c == 0, c == NC - 1)

        def multiply_last(cs):
            for c in cs:
                if c == 0:
                    accs[OT - 1] = new_acc("xb")
                mx_pass(accs[OT - 1], G + c, OT - 1, c == 0, c == NC - 1)

        xb = x_bank(0, 0, "xb")
        nc.vector.tensor_copy(out=x_cols(0, 0), in_=xb)
        xb1 = x_bank(0, 1, "acc0")
        nc.scalar.copy(out=x_cols(0, 1), in_=xb1)
        late_x = [x_bank(1, u, "acc%d" % (1 + u)) for u in range(2)]
        for h in range(2):
            periods(h, None)
        sls = [work.tile([P, CH], BF16, tag="sp", bufs=3, name="sl", align_bytes=64) for g in range(G)]

        def base_silu(g):
            nc.scalar.activation(
                out=sls[g][:].rearrange("p (c i j) -> p c j i", i=8, j=4),
                in_=xp[:, g * CH : (g + 1) * CH].rearrange("p (j c i) -> p c j i", j=4, i=8),
                func=ACT.Silu,
            )

        base_silu(0)
        xbs = []
        stretch(0, xb, (1, 0), False)
        for u in range(2):
            nc.scalar.copy(out=x_cols(1, u), in_=late_x[u])
        bankb = psum.tile([P, OT, P], BF16, tag="acc3", bufs=1, name="bankb")
        for ot in range(OT):
            nc.tensor.transpose(bankb[:, ot, :], brow[:, ot * P : (ot + 1) * P], identb[:])
        stretch(1, xb1, None, False)
        base_silu(1)
        cb = const.tile([P, OT], F32)
        nc.vector.tensor_reduce(out=cb[:], in_=bankb[:, :, 0:NF], axis=mybir.AxisListType.X, op=ALU.add)
        nc.vector.tensor_copy(out=scl[:], in_=bankb[:, :, NF])
        for c in range(RUN):
            times_coef(c, 0, TOK)
            turn(c)
            if c == 2:
                nc.vector.tensor_tensor(out=cbs[:], in0=cb[:], in1=scl[:], op=ALU.mult)
                weights_ready(1)
                for g in range(G):
                    act_tiles(g)
                    nc.vector.quantize_mx(out=sas[g][0][:].bitcast(FP8X4), scales=sas[g][1][:], in_=sls[g][:])
            pair()
            pair()
        weights_ready(2)
        base_pass(range(KEPT))
        base_exit(range(2))
        base_pass(range(KEPT, OT))

        for r in range(1, NRUN):
            stretch(2 * r, xbs[-1], (where(r * RUN)[1], 1), True)
            if r == 1:
                base_exit(range(2, OT))
            for c in range((r - 1) * RUN, r * RUN):
                quantise(c, 0, TOK)
            weights_ready(2)
            if r > 1:
                multiply_ready(2)
            stretch(2 * r + 1, xbs[-1], (where((r + 1) * RUN)[1], 0) if r < NRUN - 1 else None, True)
            if r == NRUN - 1:
                break
            for c in range(r * RUN, (r + 1) * RUN):
                times_coef(c, 0, TOK)
                turn(c)
                if c % RUN < TURN_PAIRS[r]:
                    pair()
                multiply_ready(1)
                if c % RUN >= 1:
                    weights_ready(1)

        last = NC - RUN
        multiply_ready(RUN)
        multiply_last(range(last))
        for c in range(last, NC - 1):
            times_coef(c, 0, TOK)
            turn(c)
        weights_ready(2)
        for c in (last, NC - 2, last + 1):
            quantise(c, 0, TOK)
            multiply(c)
            multiply_last([c])
            weights_ready(1)
        step = TOK // 4
        for a in range(0, TOK + step, step):
            if a < TOK:
                times_coef(NC - 1, a, a + step)
            if a > 0:
                quantise(NC - 1, a - step, a)
        multiply(NC - 1)
        multiply_last([NC - 1])

        out_view = out.rearrange("b (h p) o -> p (b h) o", p=P)
        for ot in range(OT):
            y = work.tile([P, TOK], F32, tag="y", bufs=2, name="y")
            nc.vector.scalar_tensor_tensor(
                out=y[:], in0=accs[ot][:], scalar=scl[:, ot : ot + 1], in1=base_c[:, ot, :], op0=ALU.mult, op1=ALU.add
            )
            bank = psum.tile([P, 4, P], F32, tag="tp", bufs=2, name="bank")
            for t in range(TT):
                nc.tensor.transpose(bank[:, t, :], y[:, t * P : (t + 1) * P], ident[:])
            if ot % 2 == 0:
                osb = work.tile([P, TT, 2 * P], F32, tag="sg", bufs=4, name="osb", align_bytes=64)
            nc.scalar.copy(out=osb[:, :, ot % 2 * P : (ot % 2 + 1) * P], in_=bank[:])
            if ot % 2 == 1:
                nc.sync.dma_start(out=out_view[:, :, (ot - 1) * P : (ot + 1) * P], in_=osb[:])
